import numpy as np
import ml_dtypes


def mxq(x, axis, fmt="e4m3"):
    dtype, down = {"e4m3": (ml_dtypes.float8_e4m3fn, 7), "e5m2": (ml_dtypes.float8_e5m2, 14)}[fmt]
    v = np.moveaxis(np.asarray(x, np.float32).astype(ml_dtypes.bfloat16).astype(np.float64), axis, -1)
    blocks = v.reshape(v.shape[:-1] + (-1, 32))
    amax = np.abs(blocks).max(-1, keepdims=True)
    byte = np.maximum(np.where(amax > 0, np.frexp(amax)[1] - 1 + 127, 0) - down, 1)
    scale = np.exp2(byte - 127.0)
    codes = (blocks / scale).astype(np.float32).astype(dtype).astype(np.float64)
    return np.moveaxis((codes * scale).reshape(v.shape), -1, axis)


WIDE = False


def mx_kscale(k):
    if not WIDE:
        return np.ones(k)
    levels = np.array([10, -10, 5, -5, 0])
    a = np.random.permutation(np.resize(levels, k // 512 * 4)).reshape(k // 512, 4)
    idx = np.arange(k)
    return np.exp2(a[idx // 512, idx % 128 // 32])


BF16 = ml_dtypes.bfloat16


def bf(x):
    return np.asarray(x, np.float32).astype(BF16)


def f64(x):
    return np.asarray(x).astype(np.float64)


B, N, C, H, F = 2, 512, 1024, 8, 2752
D = C // H
EPS = 1e-5


def rmsnorm(v, w):
    return v / np.sqrt(np.mean(v * v, axis=-1, keepdims=True) + EPS) * w


def setup_inputs():
    s = mx_kscale(C)
    return {"h": bf(np.random.standard_normal((B, N, C)) * s),
            "w_qk": bf(np.random.standard_normal((2 * C, C)) / np.sqrt(C) / s),
            "w_q_norm": bf(1.0 + 0.1 * np.random.standard_normal(D)),
            "w_k_norm": bf(1.0 + 0.1 * np.random.standard_normal(D))}


def reference(h, w_qk, w_q_norm, w_k_norm):
    qk = mxq(f64(h), 2, "e4m3") @ mxq(f64(w_qk), 1, "e4m3").T
    qk = qk.reshape(B, N, 2, H, D).transpose(2, 0, 3, 1, 4)
    q = rmsnorm(qk[0], f64(w_q_norm))
    k = rmsnorm(qk[1], f64(w_k_norm))
    a = (mxq(q, 2, "e4m3").transpose(0, 1, 3, 2) @ mxq(k, 2, "e4m3")) * D ** -0.5
    e = np.exp(a - a.max(-1, keepdims=True))
    return e / e.sum(-1, keepdims=True)

@@ -1,0 +1,327 @@
+from contextlib import ExitStack
+
+import concourse.mybir as mybir
+from concourse.masks import make_identity
+
+F32 = mybir.dt.float32
+BF16 = mybir.dt.bfloat16
+U32 = mybir.dt.uint32
+U8 = mybir.dt.uint8
+FP8X4 = mybir.dt.float8_e4m3fn_x4
+ACT = mybir.ActivationFunctionType
+ALU = mybir.AluOpType
+AXIS = mybir.AxisListType
+
+P = 128
+PACK = 4
+BATCH = 2
+TOKENS = 512
+CHANNELS = 1024
+PASSES = CHANNELS // (P * PACK)
+HEADS = 8
+D = 128
+EPS = 1e-5
+SOFTMAX_SCALE = D**-0.5
+
+BANK = 512
+HEADS_PER_BANK = BANK // D
+TOKEN_TILES = TOKENS // P
+WORDS = CHANNELS // 2
+HALVES = HEADS // HEADS_PER_BANK
+
+UNITS = HALVES * 2 * BATCH
+N_BANKS = UNITS * TOKEN_TILES
+ROW_TILES = (BATCH * TOKENS + 2 * HEADS * D) // P
+ROW_TILES_AHEAD = 10
+
+FLOPS = 2 * BATCH * TOKENS * CHANNELS * 2 * HEADS * D + 2 * BATCH * HEADS * D * D * TOKENS
+
+
+def tile_transposedattentiontransformer_pa_kernel(tc, h, w_qk, w_q_norm, w_k_norm, out):
+    nc = tc.nc
+    with ExitStack() as ctx:
+        const = ctx.enter_context(tc.tile_pool(name="const", bufs=1))
+        rows_pool = ctx.enter_context(tc.tile_pool(name="rows", bufs=1))
+        codes_pool = ctx.enter_context(tc.tile_pool(name="codes", bufs=1))
+        grouped_pool = ctx.enter_context(tc.tile_pool(name="grouped", bufs=2))
+        norm_pool = ctx.enter_context(tc.tile_pool(name="norm", bufs=2))
+        small = ctx.enter_context(tc.tile_pool(name="small", bufs=4))
+        soft = ctx.enter_context(tc.tile_pool(name="soft", bufs=4))
+        psum_qk = ctx.enter_context(tc.psum_pool(name="psum_qk", bufs=4))
+        psum_aux = ctx.enter_context(tc.psum_pool(name="psum_aux", bufs=4))
+        ctx.enter_context(tc.manual_schedule())
+
+        units = []
+        for half in range(HALVES):
+            for is_k in range(2):
+                for b in range(BATCH):
+                    units.append((half, is_k, b))
+
+        def chunk_of(half, is_k):
+            return is_k * HALVES + half
+
+        row_tiles = [("w", chunk_of(0, 0), i) for i in range(HEADS_PER_BANK)]
+        for b in range(BATCH):
+            row_tiles.extend([("h", b, j) for j in range(TOKEN_TILES)])
+        for half, is_k, b in units:
+            if b == 0 and (half, is_k) != (0, 0):
+                row_tiles.extend([("w", chunk_of(half, is_k), i) for i in range(HEADS_PER_BANK)])
+        assert len(row_tiles) == ROW_TILES
+
+        rows_sb = []
+        for t, (kind, group, i) in enumerate(row_tiles):
+            rows = rows_pool.tile([P, CHANNELS], BF16, name="rows%d" % t)
+            if kind == "w":
+                first = group * BANK + i * P
+                source = w_qk[first : first + P, :]
+            else:
+                source = h[group].rearrange("(p j) c -> j p c", j=TOKEN_TILES)[i]
+            nc.sync.dma_start(out=rows[:], in_=source)
+            rows_sb.append(rows)
+
+        identity = const.tile([P, P], F32)
+        make_identity(nc, identity[:])
+        eps = const.tile([P, 1], F32)
+        nc.vector.memset(eps[:], EPS)
+
+        gain_rows = const.tile([P, 2 * D], BF16)
+        nc.vector.memset(gain_rows[:], 0.0)
+        nc.scalar.dma_start(out=gain_rows[0:1, 0:D], in_=w_q_norm.rearrange("(o d) -> o d", o=1))
+        nc.scalar.dma_start(out=gain_rows[0:1, D : 2 * D], in_=w_k_norm.rearrange("(o d) -> o d", o=1))
+        warm = const.tile([P, 1], F32)
+        nc.scalar.activation(out=warm[:], in_=eps[:], func=ACT.Abs_reciprocal_sqrt)
+        ones = const.tile([P, P], BF16)
+        nc.vector.memset(ones[:], 1.0)
+        gains = const.tile([P, 2 * D], F32)
+
+        def broadcast_gains():
+            gain_ps = psum_aux.tile([P, BANK], F32, tag="aux")
+            nc.tensor.matmul(out=gain_ps[:, 0 : 2 * D], lhsT=ones[:], rhs=gain_rows[:], start=True, stop=True)
+            nc.vector.tensor_copy(out=gains[:], in_=gain_ps[:, 0 : 2 * D])
+
+        def codes_and_scales(name, width):
+            codes = codes_pool.tile([P, width], U32, name=name + "_codes", align_bytes=64)
+            scales = codes_pool.tile([P, width], U8, name=name + "_scales", align_bytes=64)
+            return codes, scales
+
+        h_mx = [codes_and_scales("h%d" % t, PASSES * P) for t in range(BATCH * TOKEN_TILES)]
+        w_mx = [[codes_and_scales("w%d_%d" % (c, g), BANK) for g in range(PASSES)] for c in range(2 * HALVES)]
+        qk_mx = [codes_and_scales("qk%d" % u, BANK) for u in range(UNITS)]
+
+        w_grouped = {}
+
+        def transpose_row_tile(t):
+            ready = []
+            kind, group, i = row_tiles[t]
+            words = rows_sb[t][:].bitcast(F32)
+            bank = psum_aux.tile([P, BANK], F32, tag="aux")
+            for block in range(WORDS // P):
+                cols = slice(block * P, (block + 1) * P)
+                nc.tensor.transpose(bank[:, cols], words[:, cols], identity[:])
+            if kind == "h":
+                grouped = grouped_pool.tile(
+                    [P, PASSES * P * PACK], BF16, name="h_grouped", bufs=4, align_bytes=64
+                )
+                target = grouped[:].bitcast(F32).rearrange("p (g r u) -> p g r u", g=PASSES, u=2)
+                ready.append(("h", group * TOKEN_TILES + i, grouped))
+            else:
+                if i == 0:
+                    w_grouped[group] = grouped_pool.tile(
+                        [P, PASSES * BANK * PACK], BF16, name="w_grouped", align_bytes=64
+                    )
+                grouped = w_grouped[group]
+                target = grouped[:].bitcast(F32).rearrange("p (g r u) -> p g r u", g=PASSES, u=2)
+                target = target[:, :, i * P : (i + 1) * P, :]
+                if i == HEADS_PER_BANK - 1:
+                    ready.append(("w", group, grouped))
+            nc.scalar.copy(out=target, in_=bank[:].rearrange("p (g u r) -> p g r u", g=PASSES, u=2))
+            return ready
+
+        def quantise_transposed(ready):
+            for kind, index, grouped in ready:
+                if kind == "h":
+                    codes, scales = h_mx[index]
+                    nc.vector.quantize_mx(out=codes[:].bitcast(FP8X4), scales=scales[:], in_=grouped[:])
+                else:
+                    for g in range(PASSES):
+                        codes, scales = w_mx[index][g]
+                        nc.vector.quantize_mx(
+                            out=codes[:].bitcast(FP8X4),
+                            scales=scales[:],
+                            in_=grouped[:, g * BANK * PACK : (g + 1) * BANK * PACK],
+                        )
+
+        raw_banks = {}
+        sum_sq_tiles = {}
+        inv_rms_tiles = {}
+        normed = {}
+        regrouped = {}
+
+        def first_matmul(n):
+            half, is_k, b = units[n // TOKEN_TILES]
+            h_codes, h_scales = h_mx[b * TOKEN_TILES + n % TOKEN_TILES]
+            raw = psum_qk.tile([P, BANK], F32, name="raw")
+            for g in range(PASSES):
+                w_codes, w_scales = w_mx[chunk_of(half, is_k)][g]
+                tokens = slice(g * P, (g + 1) * P)
+                nc.tensor.matmul_mx(
+                    out=raw[:],
+                    lhsT=h_codes[:, tokens].bitcast(FP8X4),
+                    lhsT_scale=h_scales[:, tokens],
+                    rhs=w_codes[:].bitcast(FP8X4),
+                    rhs_scale=w_scales[:],
+                    start=(g == 0),
+                    stop=(g == PASSES - 1),
+                )
+            raw_banks[n] = raw
+
+        def sum_squares(n, heads):
+            if heads[0] == 0:
+                sum_sq_tiles[n] = small.tile([P, HEADS_PER_BANK], F32, name="sum_sq")
+            for head in heads:
+                squares = small.tile([P, D], BF16, name="squares")
+                nc.scalar.activation(
+                    out=squares[:],
+                    in_=raw_banks[n][:, head * D : (head + 1) * D],
+                    func=ACT.Square,
+                    accum_out=sum_sq_tiles[n][:, head : head + 1],
+                )
+
+        def inverse_rms(n):
+            inv_rms_tiles[n] = small.tile([P, HEADS_PER_BANK], F32, name="inv_rms")
+            nc.scalar.activation(
+                out=inv_rms_tiles[n][:],
+                in_=sum_sq_tiles[n][:],
+                func=ACT.Abs_reciprocal_sqrt,
+                scale=1.0 / D,
+                bias=eps[:, 0:1],
+            )
+
+        def normalise(n):
+            u = n // TOKEN_TILES
+            j = n % TOKEN_TILES
+            is_k = units[u][1]
+            if j == 0:
+                normed[u] = norm_pool.tile([P, TOKEN_TILES * BANK], BF16, name="normed")
+            for head in range(HEADS_PER_BANK):
+                nc.vector.scalar_tensor_tensor(
+                    out=normed[u][:, j * BANK + head * D : j * BANK + (head + 1) * D],
+                    in0=raw_banks[n][:, head * D : (head + 1) * D],
+                    scalar=inv_rms_tiles[n][:, head : head + 1],
+                    in1=gains[:, is_k * D : (is_k + 1) * D],
+                    op0=ALU.mult,
+                    op1=ALU.mult,
+                )
+
+        def regroup(u):
+            regrouped[u] = norm_pool.tile([P, BANK * PACK], BF16, name="regrouped", align_bytes=64)
+            nc.vector.tensor_copy(
+                out=regrouped[u][:].rearrange("p (c i j) -> p c j i", i=4, j=TOKEN_TILES),
+                in_=normed[u][:].rearrange("p (j c i) -> p c j i", i=4, j=TOKEN_TILES),
+            )
+
+        def quantise_unit(u):
+            codes, scales = qk_mx[u]
+            nc.vector.quantize_mx(out=codes[:].bitcast(FP8X4), scales=scales[:], in_=regrouped[u][:])
+
+        scores = {}
+        neg_max = {}
+
+        def second_matmul(b, half):
+            q_codes, q_scales = qk_mx[units.index((half, 0, b))]
+            k_codes, k_scales = qk_mx[units.index((half, 1, b))]
+            bank = psum_aux.tile([P, BANK], F32, tag="aux")
+            for head in range(HEADS_PER_BANK):
+                cols = slice(head * D, (head + 1) * D)
+                nc.tensor.matmul_mx(
+                    out=bank[:, cols],
+                    lhsT=q_codes[:, cols].bitcast(FP8X4),
+                    lhsT_scale=q_scales[:, cols],
+                    rhs=k_codes[:, cols].bitcast(FP8X4),
+                    rhs_scale=k_scales[:, cols],
+                    start=True,
+                    stop=True,
+                )
+            scores[(b, half)] = bank
+
+        def softmax_max(b, half):
+            row_max = small.tile([P, HEADS_PER_BANK], F32, name="row_max")
+            nc.vector.reduce_max(
+                out=row_max[:],
+                in_=scores[(b, half)][:].rearrange("p (g e) -> p g e", g=HEADS_PER_BANK),
+                axis=AXIS.X,
+            )
+            scaled = small.tile([P, HEADS_PER_BANK], F32, name="neg_max")
+            nc.vector.tensor_scalar_mul(out=scaled[:], in0=row_max[:], scalar1=-SOFTMAX_SCALE)
+            neg_max[(b, half)] = scaled
+
+        def softmax_finish(b, half):
+            weights = soft.tile([P, BANK], F32, name="weights")
+            sums = small.tile([P, HEADS_PER_BANK], F32, name="sums")
+            for head in range(HEADS_PER_BANK):
+                cols = slice(head * D, (head + 1) * D)
+                nc.scalar.activation(
+                    out=weights[:, cols],
+                    in_=scores[(b, half)][:, cols],
+                    func=ACT.Exp,
+                    scale=SOFTMAX_SCALE,
+                    bias=neg_max[(b, half)][:, head : head + 1],
+                    accum_out=sums[:, head : head + 1],
+                )
+            inv_sums = small.tile([P, HEADS_PER_BANK], F32, name="inv_sums")
+            nc.vector.reciprocal(out=inv_sums[:], in_=sums[:])
+            for head in range(HEADS_PER_BANK):
+                cols = slice(head * D, (head + 1) * D)
+                nc.vector.tensor_scalar_mul(
+                    out=weights[:, cols], in0=weights[:, cols], scalar1=inv_sums[:, head : head + 1]
+                )
+            first_head = half * HEADS_PER_BANK
+            nc.sync.dma_start(
+                out=out[b, first_head : first_head + HEADS_PER_BANK].rearrange("g d e -> d g e"),
+                in_=weights[:].rearrange("p (g e) -> p g e", g=HEADS_PER_BANK),
+            )
+
+        first_head = [0]
+        other_heads = list(range(1, HEADS_PER_BANK))
+        ready = []
+        for n in range(-ROW_TILES_AHEAD, N_BANKS):
+            if n == 0:
+                broadcast_gains()
+            if 0 <= n + 1 < N_BANKS:
+                sum_squares(n + 1, first_head)
+            if n >= 0:
+                inverse_rms(n)
+            if 0 <= n + 1 < N_BANKS:
+                sum_squares(n + 1, other_heads)
+
+            u = n // TOKEN_TILES
+            j = n % TOKEN_TILES
+            if n >= 0:
+                normalise(n)
+            if u > 0 and j == 0:
+                regroup(u - 1)
+            if u > 0 and j == 1:
+                quantise_unit(u - 1)
+            quantise_transposed(ready)
+
+            if 0 <= n + 2 < N_BANKS:
+                first_matmul(n + 2)
+            if u > 0 and units[u - 1][1]:
+                half, is_k, b = units[u - 1]
+                if j == 2:
+                    second_matmul(b, half)
+                if j == 3:
+                    softmax_max(b, half)
+
+            ready = []
+            if n + ROW_TILES_AHEAD < ROW_TILES:
+                ready = transpose_row_tile(n + ROW_TILES_AHEAD)
+
+        regroup(UNITS - 1)
+        quantise_unit(UNITS - 1)
+        second_matmul(BATCH - 1, 1)
+        for b in range(BATCH):
+            softmax_finish(b, 0)
+        softmax_max(BATCH - 1, 1)
+        for b in range(BATCH):
+            softmax_finish(b, 1)

@@ -24,13 +24,12 @@ EPS = 1e-5
 SOFTMAX_SCALE = D**-0.5
 
 BANK = 512
-HEADS_PER_BANK = BANK // D
 TOKEN_TILES = TOKENS // P
 WORDS = CHANNELS // 2
+HEADS_PER_BANK = BANK // D
 HALVES = HEADS // HEADS_PER_BANK
 
-UNITS = HALVES * 2 * BATCH
-N_BANKS = UNITS * TOKEN_TILES
+N_BANKS = 2 * HEADS * BATCH
 ROW_TILES = (BATCH * TOKENS + 2 * HEADS * D) // P
 ROW_TILES_AHEAD = 10
 
@@ -43,36 +42,31 @@ def tile_transposedattentiontransformer_pa_kernel(tc, h, w_qk, w_q_norm, w_k_nor
         const = ctx.enter_context(tc.tile_pool(name="const", bufs=1))
         rows_pool = ctx.enter_context(tc.tile_pool(name="rows", bufs=1))
         codes_pool = ctx.enter_context(tc.tile_pool(name="codes", bufs=1))
-        grouped_pool = ctx.enter_context(tc.tile_pool(name="grouped", bufs=2))
-        norm_pool = ctx.enter_context(tc.tile_pool(name="norm", bufs=2))
-        small = ctx.enter_context(tc.tile_pool(name="small", bufs=4))
-        soft = ctx.enter_context(tc.tile_pool(name="soft", bufs=4))
+        work = ctx.enter_context(tc.tile_pool(name="work", bufs=4))
         psum_qk = ctx.enter_context(tc.psum_pool(name="psum_qk", bufs=4))
         psum_aux = ctx.enter_context(tc.psum_pool(name="psum_aux", bufs=4))
         ctx.enter_context(tc.manual_schedule())
 
-        units = []
+        banks = []
         for half in range(HALVES):
             for is_k in range(2):
                 for b in range(BATCH):
-                    units.append((half, is_k, b))
+                    for head in range(HEADS_PER_BANK):
+                        banks.append((half, is_k, b, head))
+        assert len(banks) == N_BANKS
 
-        def chunk_of(half, is_k):
-            return is_k * HALVES + half
-
-        row_tiles = [("w", chunk_of(0, 0), i) for i in range(HEADS_PER_BANK)]
-        for b in range(BATCH):
-            row_tiles.extend([("h", b, j) for j in range(TOKEN_TILES)])
-        for half, is_k, b in units:
-            if b == 0 and (half, is_k) != (0, 0):
-                row_tiles.extend([("w", chunk_of(half, is_k), i) for i in range(HEADS_PER_BANK)])
+        row_tiles = []
+        for half, is_k, b, head in banks:
+            needed = [("h", b, j) for j in range(TOKEN_TILES)]
+            needed.append(("w", is_k, half * HEADS_PER_BANK + head))
+            row_tiles.extend([key for key in needed if key not in row_tiles])
         assert len(row_tiles) == ROW_TILES
 
         rows_sb = []
         for t, (kind, group, i) in enumerate(row_tiles):
             rows = rows_pool.tile([P, CHANNELS], BF16, name="rows%d" % t)
             if kind == "w":
-                first = group * BANK + i * P
+                first = (group * HEADS + i) * D
                 source = w_qk[first : first + P, :]
             else:
                 source = h[group].rearrange("(p j) c -> j p c", j=TOKEN_TILES)[i]
@@ -104,52 +98,25 @@ def tile_transposedattentiontransformer_pa_kernel(tc, h, w_qk, w_q_norm, w_k_nor
             scales = codes_pool.tile([P, width], U8, name=name + "_scales", align_bytes=64)
             return codes, scales
 
-        h_mx = [codes_and_scales("h%d" % t, PASSES * P) for t in range(BATCH * TOKEN_TILES)]
-        w_mx = [[codes_and_scales("w%d_%d" % (c, g), BANK) for g in range(PASSES)] for c in range(2 * HALVES)]
-        qk_mx = [codes_and_scales("qk%d" % u, BANK) for u in range(UNITS)]
-
-        w_grouped = {}
+        rows_mx = [codes_and_scales("rows%d" % t, PASSES * P) for t in range(ROW_TILES)]
+        qk_mx = [codes_and_scales("qk%d" % n, D) for n in range(N_BANKS)]
 
         def transpose_row_tile(t):
-            ready = []
-            kind, group, i = row_tiles[t]
             words = rows_sb[t][:].bitcast(F32)
             bank = psum_aux.tile([P, BANK], F32, tag="aux")
             for block in range(WORDS // P):
                 cols = slice(block * P, (block + 1) * P)
                 nc.tensor.transpose(bank[:, cols], words[:, cols], identity[:])
-            if kind == "h":
-                grouped = grouped_pool.tile(
-                    [P, PASSES * P * PACK], BF16, name="h_grouped", bufs=4, align_bytes=64
-                )
-                target = grouped[:].bitcast(F32).rearrange("p (g r u) -> p g r u", g=PASSES, u=2)
-                ready.append(("h", group * TOKEN_TILES + i, grouped))
-            else:
-                if i == 0:
-                    w_grouped[group] = grouped_pool.tile(
-                        [P, PASSES * BANK * PACK], BF16, name="w_grouped", align_bytes=64
-                    )
-                grouped = w_grouped[group]
-                target = grouped[:].bitcast(F32).rearrange("p (g r u) -> p g r u", g=PASSES, u=2)
-                target = target[:, :, i * P : (i + 1) * P, :]
-                if i == HEADS_PER_BANK - 1:
-                    ready.append(("w", group, grouped))
-            nc.scalar.copy(out=target, in_=bank[:].rearrange("p (g u r) -> p g r u", g=PASSES, u=2))
-            return ready
+            grouped = work.tile([P, PASSES * P * PACK], BF16, name="grouped", align_bytes=64)
+            nc.scalar.copy(
+                out=grouped[:].bitcast(F32).rearrange("p (g r u) -> p g r u", g=PASSES, u=2),
+                in_=bank[:].rearrange("p (g u r) -> p g r u", g=PASSES, u=2),
+            )
+            return grouped
 
-        def quantise_transposed(ready):
-            for kind, index, grouped in ready:
-                if kind == "h":
-                    codes, scales = h_mx[index]
-                    nc.vector.quantize_mx(out=codes[:].bitcast(FP8X4), scales=scales[:], in_=grouped[:])
-                else:
-                    for g in range(PASSES):
-                        codes, scales = w_mx[index][g]
-                        nc.vector.quantize_mx(
-                            out=codes[:].bitcast(FP8X4),
-                            scales=scales[:],
-                            in_=grouped[:, g * BANK * PACK : (g + 1) * BANK * PACK],
-                        )
+        def quantise_row_tile(t, grouped):
+            codes, scales = rows_mx[t]
+            nc.vector.quantize_mx(out=codes[:].bitcast(FP8X4), scales=scales[:], in_=grouped[:])
 
         raw_banks = {}
         sum_sq_tiles = {}
@@ -158,37 +125,37 @@ def tile_transposedattentiontransformer_pa_kernel(tc, h, w_qk, w_q_norm, w_k_nor
         regrouped = {}
 
         def first_matmul(n):
-            half, is_k, b = units[n // TOKEN_TILES]
-            h_codes, h_scales = h_mx[b * TOKEN_TILES + n % TOKEN_TILES]
-            raw = psum_qk.tile([P, BANK], F32, name="raw")
-            for g in range(PASSES):
-                w_codes, w_scales = w_mx[chunk_of(half, is_k)][g]
-                tokens = slice(g * P, (g + 1) * P)
-                nc.tensor.matmul_mx(
-                    out=raw[:],
-                    lhsT=h_codes[:, tokens].bitcast(FP8X4),
-                    lhsT_scale=h_scales[:, tokens],
-                    rhs=w_codes[:].bitcast(FP8X4),
-                    rhs_scale=w_scales[:],
-                    start=(g == 0),
-                    stop=(g == PASSES - 1),
-                )
-            raw_banks[n] = raw
+            half, is_k, b, head = banks[n]
+            w_codes, w_scales = rows_mx[row_tiles.index(("w", is_k, half * HEADS_PER_BANK + head))]
+            raw_banks[n] = psum_qk.tile([P, BANK], F32, name="raw")
+            for j in range(TOKEN_TILES):
+                h_codes, h_scales = rows_mx[row_tiles.index(("h", b, j))]
+                for g in range(PASSES):
+                    cols = slice(g * P, (g + 1) * P)
+                    nc.tensor.matmul_mx(
+                        out=raw_banks[n][:, j * D : (j + 1) * D],
+                        lhsT=h_codes[:, cols].bitcast(FP8X4),
+                        lhsT_scale=h_scales[:, cols],
+                        rhs=w_codes[:, cols].bitcast(FP8X4),
+                        rhs_scale=w_scales[:, cols],
+                        start=(g == 0),
+                        stop=(g == PASSES - 1),
+                    )
 
-        def sum_squares(n, heads):
-            if heads[0] == 0:
-                sum_sq_tiles[n] = small.tile([P, HEADS_PER_BANK], F32, name="sum_sq")
-            for head in heads:
-                squares = small.tile([P, D], BF16, name="squares")
+        def sum_squares(n, token_tiles):
+            if token_tiles[0] == 0:
+                sum_sq_tiles[n] = work.tile([P, TOKEN_TILES], F32, name="sum_sq")
+            for j in token_tiles:
+                squares = work.tile([P, D], BF16, name="squares")
                 nc.scalar.activation(
                     out=squares[:],
-                    in_=raw_banks[n][:, head * D : (head + 1) * D],
+                    in_=raw_banks[n][:, j * D : (j + 1) * D],
                     func=ACT.Square,
-                    accum_out=sum_sq_tiles[n][:, head : head + 1],
+                    accum_out=sum_sq_tiles[n][:, j : j + 1],
                 )
 
         def inverse_rms(n):
-            inv_rms_tiles[n] = small.tile([P, HEADS_PER_BANK], F32, name="inv_rms")
+            inv_rms_tiles[n] = work.tile([P, TOKEN_TILES], F32, name="inv_rms")
             nc.scalar.activation(
                 out=inv_rms_tiles[n][:],
                 in_=sum_sq_tiles[n][:],
@@ -198,66 +165,61 @@ def tile_transposedattentiontransformer_pa_kernel(tc, h, w_qk, w_q_norm, w_k_nor
             )
 
         def normalise(n):
-            u = n // TOKEN_TILES
-            j = n % TOKEN_TILES
-            is_k = units[u][1]
-            if j == 0:
-                normed[u] = norm_pool.tile([P, TOKEN_TILES * BANK], BF16, name="normed")
-            for head in range(HEADS_PER_BANK):
+            is_k = banks[n][1]
+            normed[n] = work.tile([P, BANK], BF16, name="normed")
+            for j in range(TOKEN_TILES):
                 nc.vector.scalar_tensor_tensor(
-                    out=normed[u][:, j * BANK + head * D : j * BANK + (head + 1) * D],
-                    in0=raw_banks[n][:, head * D : (head + 1) * D],
-                    scalar=inv_rms_tiles[n][:, head : head + 1],
+                    out=normed[n][:, j * D : (j + 1) * D],
+                    in0=raw_banks[n][:, j * D : (j + 1) * D],
+                    scalar=inv_rms_tiles[n][:, j : j + 1],
                     in1=gains[:, is_k * D : (is_k + 1) * D],
                     op0=ALU.mult,
                     op1=ALU.mult,
                 )
 
-        def regroup(u):
-            regrouped[u] = norm_pool.tile([P, BANK * PACK], BF16, name="regrouped", align_bytes=64)
+        def regroup(n):
+            regrouped[n] = work.tile([P, D * PACK], BF16, name="regrouped", align_bytes=64)
             nc.vector.tensor_copy(
-                out=regrouped[u][:].rearrange("p (c i j) -> p c j i", i=4, j=TOKEN_TILES),
-                in_=normed[u][:].rearrange("p (j c i) -> p c j i", i=4, j=TOKEN_TILES),
+                out=regrouped[n][:].rearrange("p (c i j) -> p c j i", i=4, j=TOKEN_TILES),
+                in_=normed[n][:].rearrange("p (j c i) -> p c j i", i=4, j=TOKEN_TILES),
             )
 
-        def quantise_unit(u):
-            codes, scales = qk_mx[u]
-            nc.vector.quantize_mx(out=codes[:].bitcast(FP8X4), scales=scales[:], in_=regrouped[u][:])
+        def quantise(n):
+            codes, scales = qk_mx[n]
+            nc.vector.quantize_mx(out=codes[:].bitcast(FP8X4), scales=scales[:], in_=regrouped[n][:])
 
         scores = {}
         neg_max = {}
 
-        def second_matmul(b, half):
-            q_codes, q_scales = qk_mx[units.index((half, 0, b))]
-            k_codes, k_scales = qk_mx[units.index((half, 1, b))]
-            bank = psum_aux.tile([P, BANK], F32, tag="aux")
-            for head in range(HEADS_PER_BANK):
-                cols = slice(head * D, (head + 1) * D)
-                nc.tensor.matmul_mx(
-                    out=bank[:, cols],
-                    lhsT=q_codes[:, cols].bitcast(FP8X4),
-                    lhsT_scale=q_scales[:, cols],
-                    rhs=k_codes[:, cols].bitcast(FP8X4),
-                    rhs_scale=k_scales[:, cols],
-                    start=True,
-                    stop=True,
-                )
-            scores[(b, half)] = bank
+        def second_matmul(n):
+            half, is_k, b, head = banks[n]
+            q_codes, q_scales = qk_mx[banks.index((half, 0, b, head))]
+            k_codes, k_scales = qk_mx[n]
+            if head == 0:
+                scores[(b, half)] = psum_aux.tile([P, BANK], F32, name="scores", tag="aux")
+            nc.tensor.matmul_mx(
+                out=scores[(b, half)][:, head * D : (head + 1) * D],
+                lhsT=q_codes[:].bitcast(FP8X4),
+                lhsT_scale=q_scales[:],
+                rhs=k_codes[:].bitcast(FP8X4),
+                rhs_scale=k_scales[:],
+                start=True,
+                stop=True,
+            )
 
         def softmax_max(b, half):
-            row_max = small.tile([P, HEADS_PER_BANK], F32, name="row_max")
+            row_max = work.tile([P, HEADS_PER_BANK], F32, name="row_max")
             nc.vector.reduce_max(
                 out=row_max[:],
                 in_=scores[(b, half)][:].rearrange("p (g e) -> p g e", g=HEADS_PER_BANK),
                 axis=AXIS.X,
             )
-            scaled = small.tile([P, HEADS_PER_BANK], F32, name="neg_max")
-            nc.vector.tensor_scalar_mul(out=scaled[:], in0=row_max[:], scalar1=-SOFTMAX_SCALE)
-            neg_max[(b, half)] = scaled
+            neg_max[(b, half)] = work.tile([P, HEADS_PER_BANK], F32, name="neg_max")
+            nc.vector.tensor_scalar_mul(out=neg_max[(b, half)][:], in0=row_max[:], scalar1=-SOFTMAX_SCALE)
 
         def softmax_finish(b, half):
-            weights = soft.tile([P, BANK], F32, name="weights")
-            sums = small.tile([P, HEADS_PER_BANK], F32, name="sums")
+            weights = work.tile([P, BANK], F32, name="weights")
+            sums = work.tile([P, HEADS_PER_BANK], F32, name="sums")
             for head in range(HEADS_PER_BANK):
                 cols = slice(head * D, (head + 1) * D)
                 nc.scalar.activation(
@@ -268,7 +230,7 @@ def tile_transposedattentiontransformer_pa_kernel(tc, h, w_qk, w_q_norm, w_k_nor
                     bias=neg_max[(b, half)][:, head : head + 1],
                     accum_out=sums[:, head : head + 1],
                 )
-            inv_sums = small.tile([P, HEADS_PER_BANK], F32, name="inv_sums")
+            inv_sums = work.tile([P, HEADS_PER_BANK], F32, name="inv_sums")
             nc.vector.reciprocal(out=inv_sums[:], in_=sums[:])
             for head in range(HEADS_PER_BANK):
                 cols = slice(head * D, (head + 1) * D)
@@ -281,47 +243,46 @@ def tile_transposedattentiontransformer_pa_kernel(tc, h, w_qk, w_q_norm, w_k_nor
                 in_=weights[:].rearrange("p (g e) -> p g e", g=HEADS_PER_BANK),
             )
 
-        first_head = [0]
-        other_heads = list(range(1, HEADS_PER_BANK))
-        ready = []
-        for n in range(-ROW_TILES_AHEAD, N_BANKS):
+        def is_bank(n):
+            return 0 <= n < N_BANKS
+
+        def is_bank_of_k(n):
+            return is_bank(n) and banks[n][1] == 1
+
+        first_token_tile = [0]
+        other_token_tiles = list(range(1, TOKEN_TILES))
+        grouped = None
+        for n in range(-ROW_TILES_AHEAD, N_BANKS + 3):
             if n == 0:
                 broadcast_gains()
-            if 0 <= n + 1 < N_BANKS:
-                sum_squares(n + 1, first_head)
-            if n >= 0:
+            if is_bank(n + 1):
+                sum_squares(n + 1, first_token_tile)
+            if is_bank(n):
                 inverse_rms(n)
-            if 0 <= n + 1 < N_BANKS:
-                sum_squares(n + 1, other_heads)
+            if is_bank(n + 1):
+                sum_squares(n + 1, other_token_tiles)
 
-            u = n // TOKEN_TILES
-            j = n % TOKEN_TILES
-            if n >= 0:
+            if is_bank(n):
                 normalise(n)
-            if u > 0 and j == 0:
-                regroup(u - 1)
-            if u > 0 and j == 1:
-                quantise_unit(u - 1)
-            quantise_transposed(ready)
+            if is_bank(n - 1):
+                regroup(n - 1)
+            if is_bank(n - 2):
+                quantise(n - 2)
+            t = n + ROW_TILES_AHEAD
+            if grouped is not None:
+                quantise_row_tile(t - 1, grouped)
 
-            if 0 <= n + 2 < N_BANKS:
+            if is_bank(n + 2):
                 first_matmul(n + 2)
-            if u > 0 and units[u - 1][1]:
-                half, is_k, b = units[u - 1]
-                if j == 2:
-                    second_matmul(b, half)
-                if j == 3:
-                    softmax_max(b, half)
+            if is_bank_of_k(n - 3):
+                second_matmul(n - 3)
+            if is_bank_of_k(n - 4) and banks[n - 4][3] == HEADS_PER_BANK - 1:
+                softmax_max(banks[n - 4][2], banks[n - 4][0])
 
-            ready = []
-            if n + ROW_TILES_AHEAD < ROW_TILES:
-                ready = transpose_row_tile(n + ROW_TILES_AHEAD)
+            grouped = transpose_row_tile(t) if t < ROW_TILES else None
 
-        regroup(UNITS - 1)
-        quantise_unit(UNITS - 1)
-        second_matmul(BATCH - 1, 1)
-        for b in range(BATCH):
-            softmax_finish(b, 0)
-        softmax_max(BATCH - 1, 1)
-        for b in range(BATCH):
-            softmax_finish(b, 1)
+        softmax_finish(0, 0)
+        softmax_max(BATCH - 1, HALVES - 1)
+        softmax_finish(1, 0)
+        softmax_finish(0, 1)
+        softmax_finish(1, 1)

@@ -32,6 +32,7 @@ HALVES = HEADS // HEADS_PER_BANK
 N_BANKS = 2 * HEADS * BATCH
 ROW_TILES = (BATCH * TOKENS + 2 * HEADS * D) // P
 ROW_TILES_AHEAD = 10
+SCALAR_REGROUPS_EVERY = 3
 
 FLOPS = 2 * BATCH * TOKENS * CHANNELS * 2 * HEADS * D + 2 * BATCH * HEADS * D * D * TOKENS
 
@@ -107,6 +108,9 @@ def tile_transposedattentiontransformer_pa_kernel(tc, h, w_qk, w_q_norm, w_k_nor
             for block in range(WORDS // P):
                 cols = slice(block * P, (block + 1) * P)
                 nc.tensor.transpose(bank[:, cols], words[:, cols], identity[:])
+            return bank
+
+        def copy_row_tile(bank):
             grouped = work.tile([P, PASSES * P * PACK], BF16, name="grouped", align_bytes=64)
             nc.scalar.copy(
                 out=grouped[:].bitcast(F32).rearrange("p (g r u) -> p g r u", g=PASSES, u=2),
@@ -142,10 +146,9 @@ def tile_transposedattentiontransformer_pa_kernel(tc, h, w_qk, w_q_norm, w_k_nor
                         stop=(g == PASSES - 1),
                     )
 
-        def sum_squares(n, token_tiles):
-            if token_tiles[0] == 0:
-                sum_sq_tiles[n] = work.tile([P, TOKEN_TILES], F32, name="sum_sq")
-            for j in token_tiles:
+        def sum_squares(n):
+            sum_sq_tiles[n] = work.tile([P, TOKEN_TILES], F32, name="sum_sq")
+            for j in range(TOKEN_TILES):
                 squares = work.tile([P, D], BF16, name="squares")
                 nc.scalar.activation(
                     out=squares[:],
@@ -177,9 +180,9 @@ def tile_transposedattentiontransformer_pa_kernel(tc, h, w_qk, w_q_norm, w_k_nor
                     op1=ALU.mult,
                 )
 
-        def regroup(n):
+        def regroup(n, copy):
             regrouped[n] = work.tile([P, D * PACK], BF16, name="regrouped", align_bytes=64)
-            nc.vector.tensor_copy(
+            copy(
                 out=regrouped[n][:].rearrange("p (c i j) -> p c j i", i=4, j=TOKEN_TILES),
                 in_=normed[n][:].rearrange("p (j c i) -> p c j i", i=4, j=TOKEN_TILES),
             )
@@ -249,37 +252,37 @@ def tile_transposedattentiontransformer_pa_kernel(tc, h, w_qk, w_q_norm, w_k_nor
         def is_bank_of_k(n):
             return is_bank(n) and banks[n][1] == 1
 
-        first_token_tile = [0]
-        other_token_tiles = list(range(1, TOKEN_TILES))
         grouped = None
         for n in range(-ROW_TILES_AHEAD, N_BANKS + 3):
+            t = n + ROW_TILES_AHEAD
+            scalar_regroups = t >= ROW_TILES and n % SCALAR_REGROUPS_EVERY == 0
             if n == 0:
                 broadcast_gains()
-            if is_bank(n + 1):
-                sum_squares(n + 1, first_token_tile)
-            if is_bank(n):
-                inverse_rms(n)
-            if is_bank(n + 1):
-                sum_squares(n + 1, other_token_tiles)
 
-            if is_bank(n):
-                normalise(n)
-            if is_bank(n - 1):
-                regroup(n - 1)
-            if is_bank(n - 2):
-                quantise(n - 2)
-            t = n + ROW_TILES_AHEAD
             if grouped is not None:
                 quantise_row_tile(t - 1, grouped)
+            if is_bank(n):
+                normalise(n)
+            if is_bank(n - 1) and not scalar_regroups:
+                regroup(n - 1, nc.vector.tensor_copy)
+            if is_bank(n - 2):
+                quantise(n - 2)
+            if is_bank_of_k(n - 4) and banks[n - 4][3] == HEADS_PER_BANK - 1:
+                softmax_max(banks[n - 4][2], banks[n - 4][0])
 
+            transposed = transpose_row_tile(t) if t < ROW_TILES else None
             if is_bank(n + 2):
                 first_matmul(n + 2)
             if is_bank_of_k(n - 3):
                 second_matmul(n - 3)
-            if is_bank_of_k(n - 4) and banks[n - 4][3] == HEADS_PER_BANK - 1:
-                softmax_max(banks[n - 4][2], banks[n - 4][0])
 
-            grouped = transpose_row_tile(t) if t < ROW_TILES else None
+            if is_bank(n + 1):
+                sum_squares(n + 1)
+            grouped = copy_row_tile(transposed) if transposed is not None else None
+            if is_bank(n - 1) and scalar_regroups:
+                regroup(n - 1, nc.scalar.copy)
+            if is_bank(n + 1):
+                inverse_rms(n + 1)
 
         softmax_finish(0, 0)
         softmax_max(BATCH - 1, HALVES - 1)

@@ -32,7 +32,6 @@ HALVES = HEADS // HEADS_PER_BANK
 N_BANKS = 2 * HEADS * BATCH
 ROW_TILES = (BATCH * TOKENS + 2 * HEADS * D) // P
 ROW_TILES_AHEAD = 10
-SCALAR_REGROUPS_EVERY = 3
 
 FLOPS = 2 * BATCH * TOKENS * CHANNELS * 2 * HEADS * D + 2 * BATCH * HEADS * D * D * TOKENS
 
@@ -187,6 +186,9 @@ def tile_transposedattentiontransformer_pa_kernel(tc, h, w_qk, w_q_norm, w_k_nor
                 in_=normed[n][:].rearrange("p (j c i) -> p c j i", i=4, j=TOKEN_TILES),
             )
 
+        def gpsimd_copy(out, in_):
+            nc.gpsimd.tensor_scalar(out=out, in0=in_, scalar1=1.0, scalar2=0.0, op0=ALU.mult, op1=ALU.add)
+
         def quantise(n):
             codes, scales = qk_mx[n]
             nc.vector.quantize_mx(out=codes[:].bitcast(FP8X4), scales=scales[:], in_=regrouped[n][:])
@@ -255,7 +257,6 @@ def tile_transposedattentiontransformer_pa_kernel(tc, h, w_qk, w_q_norm, w_k_nor
         grouped = None
         for n in range(-ROW_TILES_AHEAD, N_BANKS + 3):
             t = n + ROW_TILES_AHEAD
-            scalar_regroups = t >= ROW_TILES and n % SCALAR_REGROUPS_EVERY == 0
             if n == 0:
                 broadcast_gains()
 
@@ -263,8 +264,8 @@ def tile_transposedattentiontransformer_pa_kernel(tc, h, w_qk, w_q_norm, w_k_nor
                 quantise_row_tile(t - 1, grouped)
             if is_bank(n):
                 normalise(n)
-            if is_bank(n - 1) and not scalar_regroups:
-                regroup(n - 1, nc.vector.tensor_copy)
+            if is_bank(n - 1):
+                regroup(n - 1, gpsimd_copy)
             if is_bank(n - 2):
                 quantise(n - 2)
             if is_bank_of_k(n - 4) and banks[n - 4][3] == HEADS_PER_BANK - 1:
@@ -279,8 +280,6 @@ def tile_transposedattentiontransformer_pa_kernel(tc, h, w_qk, w_q_norm, w_k_nor
             if is_bank(n + 1):
                 sum_squares(n + 1)
             grouped = copy_row_tile(transposed) if transposed is not None else None
-            if is_bank(n - 1) and scalar_regroups:
-                regroup(n - 1, nc.scalar.copy)
             if is_bank(n + 1):
                 inverse_rms(n + 1)
 

@@ -31,7 +31,16 @@ HALVES = HEADS // HEADS_PER_BANK
 
 N_BANKS = 2 * HEADS * BATCH
 ROW_TILES = (BATCH * TOKENS + 2 * HEADS * D) // P
-ROW_TILES_AHEAD = 10
+HALF_TILES = 2 * HEADS_PER_BANK
+
+W_AHEAD = 4
+MATMUL_AHEAD = 2
+QUANTISE_LAG = 2
+SCORES_LAG = QUANTISE_LAG + 1
+H_FIRST_STEP = 1
+LATE_W_FIRST_STEP = H_FIRST_STEP + TOKEN_TILES
+LATE_W_LAST_STEP = 2 * HALF_TILES + HALF_TILES - 1 - W_AHEAD - 2
+GPSIMD_CHANNELS = 96
 
 FLOPS = 2 * BATCH * TOKENS * CHANNELS * 2 * HEADS * D + 2 * BATCH * HEADS * D * D * TOKENS
 
@@ -42,28 +51,41 @@ def tile_transposedattentiontransformer_pa_kernel(tc, h, w_qk, w_q_norm, w_k_nor
         const = ctx.enter_context(tc.tile_pool(name="const", bufs=1))
         rows_pool = ctx.enter_context(tc.tile_pool(name="rows", bufs=1))
         codes_pool = ctx.enter_context(tc.tile_pool(name="codes", bufs=1))
-        work = ctx.enter_context(tc.tile_pool(name="work", bufs=4))
-        psum_qk = ctx.enter_context(tc.psum_pool(name="psum_qk", bufs=4))
-        psum_aux = ctx.enter_context(tc.psum_pool(name="psum_aux", bufs=4))
+        work = ctx.enter_context(tc.tile_pool(name="work", bufs=8))
+        psum = ctx.enter_context(tc.psum_pool(name="psum", bufs=8))
         ctx.enter_context(tc.manual_schedule())
 
         banks = []
         for half in range(HALVES):
-            for is_k in range(2):
-                for b in range(BATCH):
+            for b in range(BATCH):
+                for is_k in range(2):
                     for head in range(HEADS_PER_BANK):
-                        banks.append((half, is_k, b, head))
+                        banks.append((b, half, is_k, head))
         assert len(banks) == N_BANKS
 
-        row_tiles = []
-        for half, is_k, b, head in banks:
-            needed = [("h", b, j) for j in range(TOKEN_TILES)]
-            needed.append(("w", is_k, half * HEADS_PER_BANK + head))
-            row_tiles.extend([key for key in needed if key not in row_tiles])
+        def w_tile(n):
+            half, is_k, head = banks[n][1:]
+            return ("w", is_k, half * HEADS_PER_BANK + head)
+
+        first_step = -W_AHEAD - TOKEN_TILES - 1
+        tiles_of_step = {n: [] for n in range(first_step, N_BANKS + SCORES_LAG)}
+        for t, key in enumerate([w_tile(0)] + [("h", 0, j) for j in range(TOKEN_TILES)]):
+            tiles_of_step[first_step + t].append(key)
+        for n in range(1, HALF_TILES):
+            tiles_of_step[n - 1 - W_AHEAD].append(w_tile(n))
+        for j in range(TOKEN_TILES):
+            tiles_of_step[H_FIRST_STEP + j].append(("h", 1, j))
+        for i in range(HALF_TILES):
+            span = LATE_W_LAST_STEP - LATE_W_FIRST_STEP
+            tiles_of_step[LATE_W_FIRST_STEP + span * i // (HALF_TILES - 1)].append(w_tile(2 * HALF_TILES + i))
+        row_tiles = [key for n in sorted(tiles_of_step) for key in tiles_of_step[n]]
         assert len(row_tiles) == ROW_TILES
 
-        rows_sb = []
-        for t, (kind, group, i) in enumerate(row_tiles):
+        rows_sb = {}
+        gain_rows = const.tile([P, 2 * D], BF16)
+        nc.vector.memset(gain_rows[:], 0.0)
+        for t, key in enumerate(row_tiles):
+            kind, group, i = key
             rows = rows_pool.tile([P, CHANNELS], BF16, name="rows%d" % t)
             if kind == "w":
                 first = (group * HEADS + i) * D
@@ -71,17 +93,15 @@ def tile_transposedattentiontransformer_pa_kernel(tc, h, w_qk, w_q_norm, w_k_nor
             else:
                 source = h[group].rearrange("(p j) c -> j p c", j=TOKEN_TILES)[i]
             nc.sync.dma_start(out=rows[:], in_=source)
-            rows_sb.append(rows)
+            rows_sb[key] = rows
+            if key == ("h", 0, TOKEN_TILES - 1):
+                nc.sync.dma_start(out=gain_rows[0:1, 0:D], in_=w_q_norm.rearrange("(o d) -> o d", o=1))
+                nc.sync.dma_start(out=gain_rows[0:1, D : 2 * D], in_=w_k_norm.rearrange("(o d) -> o d", o=1))
 
         identity = const.tile([P, P], F32)
         make_identity(nc, identity[:])
         eps = const.tile([P, 1], F32)
         nc.vector.memset(eps[:], EPS)
-
-        gain_rows = const.tile([P, 2 * D], BF16)
-        nc.vector.memset(gain_rows[:], 0.0)
-        nc.scalar.dma_start(out=gain_rows[0:1, 0:D], in_=w_q_norm.rearrange("(o d) -> o d", o=1))
-        nc.scalar.dma_start(out=gain_rows[0:1, D : 2 * D], in_=w_k_norm.rearrange("(o d) -> o d", o=1))
         warm = const.tile([P, 1], F32)
         nc.scalar.activation(out=warm[:], in_=eps[:], func=ACT.Abs_reciprocal_sqrt)
         ones = const.tile([P, P], BF16)
@@ -89,7 +109,7 @@ def tile_transposedattentiontransformer_pa_kernel(tc, h, w_qk, w_q_norm, w_k_nor
         gains = const.tile([P, 2 * D], F32)
 
         def broadcast_gains():
-            gain_ps = psum_aux.tile([P, BANK], F32, tag="aux")
+            gain_ps = psum.tile([P, BANK], F32, tag="bank")
             nc.tensor.matmul(out=gain_ps[:, 0 : 2 * D], lhsT=ones[:], rhs=gain_rows[:], start=True, stop=True)
             nc.vector.tensor_copy(out=gains[:], in_=gain_ps[:, 0 : 2 * D])
 
@@ -98,27 +118,27 @@ def tile_transposedattentiontransformer_pa_kernel(tc, h, w_qk, w_q_norm, w_k_nor
             scales = codes_pool.tile([P, width], U8, name=name + "_scales", align_bytes=64)
             return codes, scales
 
-        rows_mx = [codes_and_scales("rows%d" % t, PASSES * P) for t in range(ROW_TILES)]
+        rows_mx = {key: codes_and_scales("rows%d" % t, PASSES * P) for t, key in enumerate(row_tiles)}
         qk_mx = [codes_and_scales("qk%d" % n, D) for n in range(N_BANKS)]
 
-        def transpose_row_tile(t):
-            words = rows_sb[t][:].bitcast(F32)
-            bank = psum_aux.tile([P, BANK], F32, tag="aux")
+        def transpose_row_tile(key):
+            words = rows_sb[key][:].bitcast(F32)
+            bank = psum.tile([P, BANK], F32, tag="bank")
             for block in range(WORDS // P):
                 cols = slice(block * P, (block + 1) * P)
                 nc.tensor.transpose(bank[:, cols], words[:, cols], identity[:])
             return bank
 
-        def copy_row_tile(bank):
+        def copy_row_tile(bank, copy):
             grouped = work.tile([P, PASSES * P * PACK], BF16, name="grouped", align_bytes=64)
-            nc.scalar.copy(
+            copy(
                 out=grouped[:].bitcast(F32).rearrange("p (g r u) -> p g r u", g=PASSES, u=2),
                 in_=bank[:].rearrange("p (g u r) -> p g r u", g=PASSES, u=2),
             )
             return grouped
 
-        def quantise_row_tile(t, grouped):
-            codes, scales = rows_mx[t]
+        def quantise_row_tile(key, grouped):
+            codes, scales = rows_mx[key]
             nc.vector.quantize_mx(out=codes[:].bitcast(FP8X4), scales=scales[:], in_=grouped[:])
 
         raw_banks = {}
@@ -127,12 +147,13 @@ def tile_transposedattentiontransformer_pa_kernel(tc, h, w_qk, w_q_norm, w_k_nor
         normed = {}
         regrouped = {}
 
-        def first_matmul(n):
-            half, is_k, b, head = banks[n]
-            w_codes, w_scales = rows_mx[row_tiles.index(("w", is_k, half * HEADS_PER_BANK + head))]
-            raw_banks[n] = psum_qk.tile([P, BANK], F32, name="raw")
-            for j in range(TOKEN_TILES):
-                h_codes, h_scales = rows_mx[row_tiles.index(("h", b, j))]
+        def first_matmul(n, tokens=range(TOKEN_TILES)):
+            b = banks[n][0]
+            w_codes, w_scales = rows_mx[w_tile(n)]
+            if n not in raw_banks:
+                raw_banks[n] = psum.tile([P, BANK], F32, name="raw", tag="bank")
+            for j in tokens:
+                h_codes, h_scales = rows_mx[("h", b, j)]
                 for g in range(PASSES):
                     cols = slice(g * P, (g + 1) * P)
                     nc.tensor.matmul_mx(
@@ -145,9 +166,10 @@ def tile_transposedattentiontransformer_pa_kernel(tc, h, w_qk, w_q_norm, w_k_nor
                         stop=(g == PASSES - 1),
                     )
 
-        def sum_squares(n):
-            sum_sq_tiles[n] = work.tile([P, TOKEN_TILES], F32, name="sum_sq")
-            for j in range(TOKEN_TILES):
+        def sum_squares(n, tokens=range(TOKEN_TILES)):
+            if n not in sum_sq_tiles:
+                sum_sq_tiles[n] = work.tile([P, TOKEN_TILES], F32, name="sum_sq")
+            for j in tokens:
                 squares = work.tile([P, D], BF16, name="squares")
                 nc.scalar.activation(
                     out=squares[:],
@@ -167,7 +189,7 @@ def tile_transposedattentiontransformer_pa_kernel(tc, h, w_qk, w_q_norm, w_k_nor
             )
 
         def normalise(n):
-            is_k = banks[n][1]
+            is_k = banks[n][2]
             normed[n] = work.tile([P, BANK], BF16, name="normed")
             for j in range(TOKEN_TILES):
                 nc.vector.scalar_tensor_tensor(
@@ -178,32 +200,42 @@ def tile_transposedattentiontransformer_pa_kernel(tc, h, w_qk, w_q_norm, w_k_nor
                     op0=ALU.mult,
                     op1=ALU.mult,
                 )
-
-        def regroup(n, copy):
             regrouped[n] = work.tile([P, D * PACK], BF16, name="regrouped", align_bytes=64)
-            copy(
-                out=regrouped[n][:].rearrange("p (c i j) -> p c j i", i=4, j=TOKEN_TILES),
-                in_=normed[n][:].rearrange("p (j c i) -> p c j i", i=4, j=TOKEN_TILES),
-            )
 
         def gpsimd_copy(out, in_):
             nc.gpsimd.tensor_scalar(out=out, in0=in_, scalar1=1.0, scalar2=0.0, op0=ALU.mult, op1=ALU.add)
+
+        def regroup(n, copy, first, last):
+            chans = slice(first, last)
+            copy(
+                out=regrouped[n][:, first * PACK : last * PACK].rearrange("p (c i j) -> p c j i", i=4, j=TOKEN_TILES),
+                in_=normed[n][:].rearrange("p (j c) -> p j c", j=TOKEN_TILES)[:, :, chans].rearrange(
+                    "p j (c i) -> p c j i", i=4
+                ),
+            )
 
         def quantise(n):
             codes, scales = qk_mx[n]
             nc.vector.quantize_mx(out=codes[:].bitcast(FP8X4), scales=scales[:], in_=regrouped[n][:])
 
         scores = {}
+        head_scores = {}
+        row_max = {}
         neg_max = {}
 
         def second_matmul(n):
-            half, is_k, b, head = banks[n]
-            q_codes, q_scales = qk_mx[banks.index((half, 0, b, head))]
+            b, half, is_k, head = banks[n]
+            q_codes, q_scales = qk_mx[banks.index((b, half, 0, head))]
             k_codes, k_scales = qk_mx[n]
+            apart = n >= N_BANKS - HEADS_PER_BANK
+            if head == 0 or apart:
+                bank_of_scores = psum.tile([P, BANK], F32, name="scores", tag="bank")
             if head == 0:
-                scores[(b, half)] = psum_aux.tile([P, BANK], F32, name="scores", tag="aux")
+                scores[(b, half)] = bank_of_scores
+            first = 0 if apart else head * D
+            head_scores[(b, half, head)] = (bank_of_scores if apart else scores[(b, half)])[:, first : first + D]
             nc.tensor.matmul_mx(
-                out=scores[(b, half)][:, head * D : (head + 1) * D],
+                out=head_scores[(b, half, head)],
                 lhsT=q_codes[:].bitcast(FP8X4),
                 lhsT_scale=q_scales[:],
                 rhs=k_codes[:].bitcast(FP8X4),
@@ -212,79 +244,144 @@ def tile_transposedattentiontransformer_pa_kernel(tc, h, w_qk, w_q_norm, w_k_nor
                 stop=True,
             )
 
-        def softmax_max(b, half):
-            row_max = work.tile([P, HEADS_PER_BANK], F32, name="row_max")
+        def softmax_max(b, half, heads=slice(0, HEADS_PER_BANK)):
+            count = heads.stop - heads.start
+            if (b, half) not in row_max:
+                row_max[(b, half)] = work.tile([P, HEADS_PER_BANK], F32, name="row_max")
+                neg_max[(b, half)] = work.tile([P, HEADS_PER_BANK], F32, name="neg_max")
             nc.vector.reduce_max(
-                out=row_max[:],
-                in_=scores[(b, half)][:].rearrange("p (g e) -> p g e", g=HEADS_PER_BANK),
+                out=row_max[(b, half)][:, heads],
+                in_=scores[(b, half)][:, heads.start * D : heads.stop * D].rearrange("p (g e) -> p g e", g=count),
                 axis=AXIS.X,
             )
-            neg_max[(b, half)] = work.tile([P, HEADS_PER_BANK], F32, name="neg_max")
-            nc.vector.tensor_scalar_mul(out=neg_max[(b, half)][:], in0=row_max[:], scalar1=-SOFTMAX_SCALE)
 
-        def softmax_finish(b, half):
-            weights = work.tile([P, BANK], F32, name="weights")
-            sums = work.tile([P, HEADS_PER_BANK], F32, name="sums")
-            for head in range(HEADS_PER_BANK):
+        def softmax_negate(b, half, heads=slice(0, HEADS_PER_BANK)):
+            nc.vector.tensor_scalar_mul(out=neg_max[(b, half)][:, heads], in0=row_max[(b, half)][:, heads], scalar1=-SOFTMAX_SCALE)
+
+        def softmax_shift(b, half, head):
+            if (b, half) not in neg_max:
+                neg_max[(b, half)] = work.tile([P, HEADS_PER_BANK], F32, name="neg_max")
+            junk = work.tile([P, D], F32, name="junk")
+            nc.vector.tensor_scalar(
+                out=junk[:],
+                in0=head_scores[(b, half, head)],
+                scalar1=-SOFTMAX_SCALE,
+                scalar2=None,
+                op0=ALU.mult,
+                op1=ALU.min,
+                accum_out=neg_max[(b, half)][:, head : head + 1],
+            )
+
+        weights = {}
+        sums = {}
+        inv_sums = {}
+
+        def softmax_exp(b, half, heads=slice(0, HEADS_PER_BANK)):
+            key = (b, half)
+            if key not in weights:
+                weights[key] = work.tile([P, BANK], F32, name="weights")
+                sums[key] = work.tile([P, HEADS_PER_BANK], F32, name="sums")
+                inv_sums[key] = work.tile([P, HEADS_PER_BANK], F32, name="inv_sums")
+            for head in range(heads.start, heads.stop):
                 cols = slice(head * D, (head + 1) * D)
                 nc.scalar.activation(
-                    out=weights[:, cols],
-                    in_=scores[(b, half)][:, cols],
+                    out=weights[key][:, cols],
+                    in_=head_scores[(b, half, head)],
                     func=ACT.Exp,
                     scale=SOFTMAX_SCALE,
-                    bias=neg_max[(b, half)][:, head : head + 1],
-                    accum_out=sums[:, head : head + 1],
+                    bias=neg_max[key][:, head : head + 1],
+                    accum_out=sums[key][:, head : head + 1],
                 )
-            inv_sums = work.tile([P, HEADS_PER_BANK], F32, name="inv_sums")
-            nc.vector.reciprocal(out=inv_sums[:], in_=sums[:])
-            for head in range(HEADS_PER_BANK):
+
+        def softmax_recip(b, half, heads=slice(0, HEADS_PER_BANK)):
+            key = (b, half)
+            nc.vector.reciprocal(out=inv_sums[key][:, heads], in_=sums[key][:, heads])
+
+        def softmax_mul(b, half, heads=slice(0, HEADS_PER_BANK)):
+            key = (b, half)
+            for head in range(heads.start, heads.stop):
                 cols = slice(head * D, (head + 1) * D)
                 nc.vector.tensor_scalar_mul(
-                    out=weights[:, cols], in0=weights[:, cols], scalar1=inv_sums[:, head : head + 1]
+                    out=weights[key][:, cols], in0=weights[key][:, cols], scalar1=inv_sums[key][:, head : head + 1]
                 )
-            first_head = half * HEADS_PER_BANK
+            first = half * HEADS_PER_BANK
             nc.sync.dma_start(
-                out=out[b, first_head : first_head + HEADS_PER_BANK].rearrange("g d e -> d g e"),
-                in_=weights[:].rearrange("p (g e) -> p g e", g=HEADS_PER_BANK),
+                out=out[b, first + heads.start : first + heads.stop].rearrange("g d e -> d g e"),
+                in_=weights[key][:, heads.start * D : heads.stop * D].rearrange("p (g e) -> p g e", g=heads.stop - heads.start),
             )
 
         def is_bank(n):
             return 0 <= n < N_BANKS
 
         def is_bank_of_k(n):
-            return is_bank(n) and banks[n][1] == 1
+            return is_bank(n) and banks[n][2] == 1
 
-        grouped = None
-        for n in range(-ROW_TILES_AHEAD, N_BANKS + 3):
-            t = n + ROW_TILES_AHEAD
-            if n == 0:
+        last_banks = range(N_BANKS - HEADS_PER_BANK, N_BANKS)
+        scores_done = [banks[n][:2] for n in range(N_BANKS) if is_bank_of_k(n) and banks[n][3] == HEADS_PER_BANK - 1]
+        early_scores, last_scores = scores_done[:-1], scores_done[-1]
+        last_head = HEADS_PER_BANK - 1
+        exps = list(early_scores)
+
+        copied = []
+        for n in range(first_step, N_BANKS + SCORES_LAG):
+            if n == -MATMUL_AHEAD:
                 broadcast_gains()
+            tiles = tiles_of_step[n]
+            in_psum = [transpose_row_tile(key) for key in tiles]
+            newly_copied = []
+            squares_left = n + 1 < N_BANKS
 
-            if grouped is not None:
-                quantise_row_tile(t - 1, grouped)
             if is_bank(n):
                 normalise(n)
-            if is_bank(n - 1):
-                regroup(n - 1, gpsimd_copy)
-            if is_bank(n - 2):
-                quantise(n - 2)
-            if is_bank_of_k(n - 4) and banks[n - 4][3] == HEADS_PER_BANK - 1:
-                softmax_max(banks[n - 4][2], banks[n - 4][0])
+            for key, bank in zip(tiles[1:], in_psum[1:]):
+                newly_copied.append((key, copy_row_tile(bank, nc.vector.tensor_copy)))
+            m = n - SCORES_LAG - 1
+            if is_bank_of_k(m) and m in last_banks:
+                softmax_shift(*banks[m][:2], banks[m][3])
+            elif is_bank_of_k(m) and banks[m][3] == last_head:
+                softmax_max(*banks[m][:2])
+            if is_bank(n - 1) and not squares_left:
+                regroup(n - 1, nc.vector.tensor_copy, GPSIMD_CHANNELS if is_bank(n) else 0, D)
+            for key, grouped in copied:
+                quantise_row_tile(key, grouped)
+            if is_bank(n - QUANTISE_LAG):
+                quantise(n - QUANTISE_LAG)
+            if is_bank_of_k(m) and m not in last_banks and banks[m][3] == last_head:
+                softmax_negate(*banks[m][:2])
 
-            transposed = transpose_row_tile(t) if t < ROW_TILES else None
-            if is_bank(n + 2):
-                first_matmul(n + 2)
-            if is_bank_of_k(n - 3):
-                second_matmul(n - 3)
+            if is_bank(n + MATMUL_AHEAD):
+                first_matmul(n + MATMUL_AHEAD)
+            if is_bank_of_k(n - SCORES_LAG):
+                second_matmul(n - SCORES_LAG)
 
             if is_bank(n + 1):
                 sum_squares(n + 1)
-            grouped = copy_row_tile(transposed) if transposed is not None else None
+            for key, bank in zip(tiles[:1], in_psum[:1]):
+                newly_copied.append((key, copy_row_tile(bank, nc.scalar.copy)))
+            if is_bank(n - 1) and squares_left:
+                regroup(n - 1, nc.scalar.copy, GPSIMD_CHANNELS, D)
             if is_bank(n + 1):
                 inverse_rms(n + 1)
+            elif n >= N_BANKS - 1 and exps:
+                softmax_exp(*exps.pop(0))
 
-        softmax_finish(0, 0)
-        softmax_max(BATCH - 1, HALVES - 1)
-        softmax_finish(1, 0)
-        softmax_finish(0, 1)
-        softmax_finish(1, 1)
+            if is_bank(n - 1) and is_bank(n):
+                regroup(n - 1, gpsimd_copy, 0, GPSIMD_CHANNELS)
+
+            copied = newly_copied
+
+        most = slice(0, last_head)
+        one = slice(last_head, HEADS_PER_BANK)
+        softmax_recip(*early_scores[0])
+        softmax_recip(*early_scores[1])
+        softmax_exp(*last_scores, heads=most)
+        softmax_mul(*early_scores[0])
+        softmax_shift(*last_scores, last_head)
+        softmax_exp(*last_scores, heads=one)
+        softmax_mul(*early_scores[1])
+        softmax_recip(*early_scores[2])
+        softmax_recip(*last_scores, heads=most)
+        softmax_mul(*early_scores[2])
+        softmax_mul(*last_scores, heads=most)
+        softmax_recip(*last_scores, heads=one)
+        softmax_mul(*last_scores, heads=one)

@@ -36,11 +36,11 @@ HALF_TILES = 2 * HEADS_PER_BANK
 W_AHEAD = 4
 MATMUL_AHEAD = 2
 QUANTISE_LAG = 2
-SCORES_LAG = QUANTISE_LAG + 1
+SCORES_LAG = QUANTISE_LAG + 2
 H_FIRST_STEP = 1
 LATE_W_FIRST_STEP = H_FIRST_STEP + TOKEN_TILES
 LATE_W_LAST_STEP = 2 * HALF_TILES + HALF_TILES - 1 - W_AHEAD - 2
-GPSIMD_CHANNELS = 96
+GPSIMD_CHANNELS = 80
 
 FLOPS = 2 * BATCH * TOKENS * CHANNELS * 2 * HEADS * D + 2 * BATCH * HEADS * D * D * TOKENS
 
@@ -322,8 +322,12 @@ def tile_transposedattentiontransformer_pa_kernel(tc, h, w_qk, w_q_norm, w_k_nor
         last_head = HEADS_PER_BANK - 1
         exps = list(early_scores)
 
+        deferred = None
+        def on_vector(n, i):
+            return i == 1 or (n < 0 and n % 2 == 1)
+
         copied = []
-        for n in range(first_step, N_BANKS + SCORES_LAG):
+        for n in range(first_step, N_BANKS):
             if n == -MATMUL_AHEAD:
                 broadcast_gains()
             tiles = tiles_of_step[n]
@@ -331,22 +335,28 @@ def tile_transposedattentiontransformer_pa_kernel(tc, h, w_qk, w_q_norm, w_k_nor
             newly_copied = []
             squares_left = n + 1 < N_BANKS
 
+            if is_bank(n + 1):
+                sum_squares(n + 1, [0])
+            if deferred is not None:
+                inverse_rms(deferred)
+                deferred = None
             if is_bank(n):
                 normalise(n)
-            for key, bank in zip(tiles[1:], in_psum[1:]):
+            for i, (key, bank) in enumerate(zip(tiles, in_psum)):
+                if not on_vector(n, i):
+                    continue
                 newly_copied.append((key, copy_row_tile(bank, nc.vector.tensor_copy)))
             m = n - SCORES_LAG - 1
-            if is_bank_of_k(m) and m in last_banks:
-                softmax_shift(*banks[m][:2], banks[m][3])
-            elif is_bank_of_k(m) and banks[m][3] == last_head:
+            if is_bank_of_k(m) and banks[m][3] == last_head:
                 softmax_max(*banks[m][:2])
-            if is_bank(n - 1) and not squares_left:
-                regroup(n - 1, nc.vector.tensor_copy, GPSIMD_CHANNELS if is_bank(n) else 0, D)
+            vector_helps = not squares_left or n % 2 == 0
+            if is_bank(n - 1) and vector_helps:
+                regroup(n - 1, nc.vector.tensor_copy, GPSIMD_CHANNELS, D)
             for key, grouped in copied:
                 quantise_row_tile(key, grouped)
             if is_bank(n - QUANTISE_LAG):
                 quantise(n - QUANTISE_LAG)
-            if is_bank_of_k(m) and m not in last_banks and banks[m][3] == last_head:
+            if is_bank_of_k(m) and banks[m][3] == last_head:
                 softmax_negate(*banks[m][:2])
 
             if is_bank(n + MATMUL_AHEAD):
@@ -355,33 +365,52 @@ def tile_transposedattentiontransformer_pa_kernel(tc, h, w_qk, w_q_norm, w_k_nor
                 second_matmul(n - SCORES_LAG)
 
             if is_bank(n + 1):
-                sum_squares(n + 1)
-            for key, bank in zip(tiles[:1], in_psum[:1]):
+                sum_squares(n + 1, [1, 2, 3])
+            for i, (key, bank) in enumerate(zip(tiles, in_psum)):
+                if on_vector(n, i):
+                    continue
                 newly_copied.append((key, copy_row_tile(bank, nc.scalar.copy)))
-            if is_bank(n - 1) and squares_left:
+            if is_bank(n - 1) and not vector_helps:
                 regroup(n - 1, nc.scalar.copy, GPSIMD_CHANNELS, D)
             if is_bank(n + 1):
-                inverse_rms(n + 1)
+                if tiles or n + 2 >= N_BANKS or (squares_left and is_bank(n - 1) and not vector_helps):
+                    inverse_rms(n + 1)
+                else:
+                    deferred = n + 1
             elif n >= N_BANKS - 1 and exps:
                 softmax_exp(*exps.pop(0))
 
-            if is_bank(n - 1) and is_bank(n):
+            if is_bank(n - 1):
                 regroup(n - 1, gpsimd_copy, 0, GPSIMD_CHANNELS)
 
             copied = newly_copied
 
         most = slice(0, last_head)
         one = slice(last_head, HEADS_PER_BANK)
-        softmax_recip(*early_scores[0])
-        softmax_recip(*early_scores[1])
+        n = N_BANKS - 1
+        d0, d1, d2 = early_scores
+        for key in exps:
+            softmax_exp(*key)
+        second_matmul(n - 3)
+        second_matmul(n - 2)
+        regroup(n, nc.vector.tensor_copy, 0, D)
+        quantise(n - 1)
+        second_matmul(n - 1)
+        softmax_shift(*last_scores, 0)
+        quantise(n)
+        second_matmul(n)
+        softmax_shift(*last_scores, 1)
+        softmax_recip(*d0)
+        softmax_shift(*last_scores, 2)
         softmax_exp(*last_scores, heads=most)
-        softmax_mul(*early_scores[0])
-        softmax_shift(*last_scores, last_head)
+        softmax_mul(*d0)
+        softmax_shift(*last_scores, 3)
         softmax_exp(*last_scores, heads=one)
-        softmax_mul(*early_scores[1])
-        softmax_recip(*early_scores[2])
+        softmax_recip(*d1)
+        softmax_recip(*d2)
+        softmax_mul(*d1)
         softmax_recip(*last_scores, heads=most)
-        softmax_mul(*early_scores[2])
-        softmax_mul(*last_scores, heads=most)
+        softmax_mul(*d2)
         softmax_recip(*last_scores, heads=one)
+        softmax_mul(*last_scores, heads=most)
         softmax_mul(*last_scores, heads=one)

@@ -33,14 +33,16 @@ N_BANKS = 2 * HEADS * BATCH
 ROW_TILES = (BATCH * TOKENS + 2 * HEADS * D) // P
 HALF_TILES = 2 * HEADS_PER_BANK
 
-W_AHEAD = 4
 MATMUL_AHEAD = 2
 QUANTISE_LAG = 2
 SCORES_LAG = QUANTISE_LAG + 2
-H_FIRST_STEP = 1
-LATE_W_FIRST_STEP = H_FIRST_STEP + TOKEN_TILES
-LATE_W_LAST_STEP = 2 * HALF_TILES + HALF_TILES - 1 - W_AHEAD - 2
-GPSIMD_CHANNELS = 80
+FIRST_STEP = -9
+SINGLE_TILES = 4
+PAIRS_FIRST_STEP = FIRST_STEP + SINGLE_TILES
+PAIRS_LAST_STEP = HALF_TILES - MATMUL_AHEAD - 2
+LATE_FIRST_STEP = PAIRS_LAST_STEP + 1
+GPSIMD_CHANNELS = 88
+ROW_TILES_DONE = 2 * HALF_TILES
 
 FLOPS = 2 * BATCH * TOKENS * CHANNELS * 2 * HEADS * D + 2 * BATCH * HEADS * D * D * TOKENS
 
@@ -67,17 +69,17 @@ def tile_transposedattentiontransformer_pa_kernel(tc, h, w_qk, w_q_norm, w_k_nor
             half, is_k, head = banks[n][1:]
             return ("w", is_k, half * HEADS_PER_BANK + head)
 
-        first_step = -W_AHEAD - TOKEN_TILES - 1
-        tiles_of_step = {n: [] for n in range(first_step, N_BANKS + SCORES_LAG)}
-        for t, key in enumerate([w_tile(0)] + [("h", 0, j) for j in range(TOKEN_TILES)]):
-            tiles_of_step[first_step + t].append(key)
-        for n in range(1, HALF_TILES):
-            tiles_of_step[n - 1 - W_AHEAD].append(w_tile(n))
-        for j in range(TOKEN_TILES):
-            tiles_of_step[H_FIRST_STEP + j].append(("h", 1, j))
+        tiles_of_step = {n: [] for n in range(FIRST_STEP, N_BANKS)}
+        early_tiles = [w_tile(0)] + [("h", 0, j) for j in range(TOKEN_TILES)]
+        early_tiles += [w_tile(n) for n in range(1, HALF_TILES)] + [("h", 1, j) for j in range(TOKEN_TILES)]
+        for t, key in enumerate(early_tiles):
+            if t < SINGLE_TILES:
+                step = FIRST_STEP + t
+            else:
+                step = min(PAIRS_FIRST_STEP + 2 * ((t - SINGLE_TILES) // 2), PAIRS_LAST_STEP)
+            tiles_of_step[step].append(key)
         for i in range(HALF_TILES):
-            span = LATE_W_LAST_STEP - LATE_W_FIRST_STEP
-            tiles_of_step[LATE_W_FIRST_STEP + span * i // (HALF_TILES - 1)].append(w_tile(2 * HALF_TILES + i))
+            tiles_of_step[LATE_FIRST_STEP + i // 2 * 3 + i % 2].append(w_tile(2 * HALF_TILES + i))
         row_tiles = [key for n in sorted(tiles_of_step) for key in tiles_of_step[n]]
         assert len(row_tiles) == ROW_TILES
 
@@ -324,10 +326,10 @@ def tile_transposedattentiontransformer_pa_kernel(tc, h, w_qk, w_q_norm, w_k_nor
 
         deferred = None
         def on_vector(n, i):
-            return i == 1 or (n < 0 and n % 2 == 1)
+            return i == 1 and n < PAIRS_LAST_STEP
 
         copied = []
-        for n in range(first_step, N_BANKS):
+        for n in range(FIRST_STEP, N_BANKS):
             if n == -MATMUL_AHEAD:
                 broadcast_gains()
             tiles = tiles_of_step[n]
@@ -349,7 +351,7 @@ def tile_transposedattentiontransformer_pa_kernel(tc, h, w_qk, w_q_norm, w_k_nor
             m = n - SCORES_LAG - 1
             if is_bank_of_k(m) and banks[m][3] == last_head:
                 softmax_max(*banks[m][:2])
-            vector_helps = not squares_left or n % 2 == 0
+            vector_helps = not squares_left or (n % 3 != 0 if n < ROW_TILES_DONE else n % 3 == 0)
             if is_bank(n - 1) and vector_helps:
                 regroup(n - 1, nc.vector.tensor_copy, GPSIMD_CHANNELS, D)
             for key, grouped in copied:
@@ -396,9 +398,9 @@ def tile_transposedattentiontransformer_pa_kernel(tc, h, w_qk, w_q_norm, w_k_nor
         regroup(n, nc.vector.tensor_copy, 0, D)
         quantise(n - 1)
         second_matmul(n - 1)
-        softmax_shift(*last_scores, 0)
         quantise(n)
         second_matmul(n)
+        softmax_shift(*last_scores, 0)
         softmax_shift(*last_scores, 1)
         softmax_recip(*d0)
         softmax_shift(*last_scores, 2)

@@ -351,7 +351,7 @@ def tile_transposedattentiontransformer_pa_kernel(tc, h, w_qk, w_q_norm, w_k_nor
             m = n - SCORES_LAG - 1
             if is_bank_of_k(m) and banks[m][3] == last_head:
                 softmax_max(*banks[m][:2])
-            vector_helps = not squares_left or (n % 3 != 0 if n < ROW_TILES_DONE else n % 3 == 0)
+            vector_helps = not squares_left or ((n % 3 != 0 if n < ROW_TILES_DONE else n % 3 == 0))
             if is_bank(n - 1) and vector_helps:
                 regroup(n - 1, nc.vector.tensor_copy, GPSIMD_CHANNELS, D)
             for key, grouped in copied:
@@ -375,7 +375,7 @@ def tile_transposedattentiontransformer_pa_kernel(tc, h, w_qk, w_q_norm, w_k_nor
             if is_bank(n - 1) and not vector_helps:
                 regroup(n - 1, nc.scalar.copy, GPSIMD_CHANNELS, D)
             if is_bank(n + 1):
-                if tiles or n + 2 >= N_BANKS or (squares_left and is_bank(n - 1) and not vector_helps):
+                if tiles or n + 2 >= N_BANKS:
                     inverse_rms(n + 1)
                 else:
                     deferred = n + 1

@@ -37,11 +37,11 @@ MATMUL_AHEAD = 2
 QUANTISE_LAG = 2
 SCORES_LAG = QUANTISE_LAG + 2
 FIRST_STEP = -9
-SINGLE_TILES = 4
+SINGLE_TILES = TOKEN_TILES + 2
 PAIRS_FIRST_STEP = FIRST_STEP + SINGLE_TILES
 PAIRS_LAST_STEP = HALF_TILES - MATMUL_AHEAD - 2
 LATE_FIRST_STEP = PAIRS_LAST_STEP + 1
-GPSIMD_CHANNELS = 88
+GPSIMD_CHANNELS = 92
 ROW_TILES_DONE = 2 * HALF_TILES
 
 FLOPS = 2 * BATCH * TOKENS * CHANNELS * 2 * HEADS * D + 2 * BATCH * HEADS * D * D * TOKENS
@@ -79,7 +79,7 @@ def tile_transposedattentiontransformer_pa_kernel(tc, h, w_qk, w_q_norm, w_k_nor
                 step = min(PAIRS_FIRST_STEP + 2 * ((t - SINGLE_TILES) // 2), PAIRS_LAST_STEP)
             tiles_of_step[step].append(key)
         for i in range(HALF_TILES):
-            tiles_of_step[LATE_FIRST_STEP + i // 2 * 3 + i % 2].append(w_tile(2 * HALF_TILES + i))
+            tiles_of_step[LATE_FIRST_STEP + 8 * i // 5].append(w_tile(2 * HALF_TILES + i))
         row_tiles = [key for n in sorted(tiles_of_step) for key in tiles_of_step[n]]
         assert len(row_tiles) == ROW_TILES
 
@@ -344,21 +344,19 @@ def tile_transposedattentiontransformer_pa_kernel(tc, h, w_qk, w_q_norm, w_k_nor
                 deferred = None
             if is_bank(n):
                 normalise(n)
+            for key, grouped in copied:
+                quantise_row_tile(key, grouped)
+            vector_helps = not squares_left or (n % 3 != 0 if n < ROW_TILES_DONE else n % 3 == 0)
+            if is_bank(n - 1) and vector_helps:
+                regroup(n - 1, nc.vector.tensor_copy, GPSIMD_CHANNELS, D)
             for i, (key, bank) in enumerate(zip(tiles, in_psum)):
-                if not on_vector(n, i):
-                    continue
-                newly_copied.append((key, copy_row_tile(bank, nc.vector.tensor_copy)))
+                if on_vector(n, i):
+                    newly_copied.append((key, copy_row_tile(bank, nc.vector.tensor_copy)))
+            if is_bank(n - QUANTISE_LAG):
+                quantise(n - QUANTISE_LAG)
             m = n - SCORES_LAG - 1
             if is_bank_of_k(m) and banks[m][3] == last_head:
                 softmax_max(*banks[m][:2])
-            vector_helps = not squares_left or ((n % 3 != 0 if n < ROW_TILES_DONE else n % 3 == 0))
-            if is_bank(n - 1) and vector_helps:
-                regroup(n - 1, nc.vector.tensor_copy, GPSIMD_CHANNELS, D)
-            for key, grouped in copied:
-                quantise_row_tile(key, grouped)
-            if is_bank(n - QUANTISE_LAG):
-                quantise(n - QUANTISE_LAG)
-            if is_bank_of_k(m) and banks[m][3] == last_head:
                 softmax_negate(*banks[m][:2])
 
             if is_bank(n + MATMUL_AHEAD):
@@ -400,19 +398,19 @@ def tile_transposedattentiontransformer_pa_kernel(tc, h, w_qk, w_q_norm, w_k_nor
         second_matmul(n - 1)
         quantise(n)
         second_matmul(n)
-        softmax_shift(*last_scores, 0)
-        softmax_shift(*last_scores, 1)
         softmax_recip(*d0)
+        softmax_shift(*last_scores, 0)
+        softmax_mul(*d0)
+        softmax_shift(*last_scores, 1)
+        softmax_recip(*d1)
         softmax_shift(*last_scores, 2)
         softmax_exp(*last_scores, heads=most)
-        softmax_mul(*d0)
+        softmax_mul(*d1)
         softmax_shift(*last_scores, 3)
         softmax_exp(*last_scores, heads=one)
-        softmax_recip(*d1)
         softmax_recip(*d2)
-        softmax_mul(*d1)
-        softmax_recip(*last_scores, heads=most)
         softmax_mul(*d2)
-        softmax_recip(*last_scores, heads=one)
+        softmax_recip(*last_scores, heads=most)
         softmax_mul(*last_scores, heads=most)
+        softmax_recip(*last_scores, heads=one)
         softmax_mul(*last_scores, heads=one)

@@ -108,12 +108,21 @@ def tile_transposedattentiontransformer_pa_kernel(tc, h, w_qk, w_q_norm, w_k_nor
         nc.scalar.activation(out=warm[:], in_=eps[:], func=ACT.Abs_reciprocal_sqrt)
         ones = const.tile([P, P], BF16)
         nc.vector.memset(ones[:], 1.0)
+        zeros = const.tile([P, BANK], BF16)
+        nc.vector.memset(zeros[:], 0.0)
         gains = const.tile([P, 2 * D], F32)
 
         def broadcast_gains():
             gain_ps = psum.tile([P, BANK], F32, tag="bank")
             nc.tensor.matmul(out=gain_ps[:, 0 : 2 * D], lhsT=ones[:], rhs=gain_rows[:], start=True, stop=True)
             nc.vector.tensor_copy(out=gains[:], in_=gain_ps[:, 0 : 2 * D])
+
+        def keep_clock(columns, times=1):
+            unread = psum.tile([P, BANK], F32, tag="bank")
+            for i in range(times):
+                nc.tensor.matmul(
+                    out=unread[:, 0:columns], lhsT=ones[:], rhs=zeros[:, 0:columns], start=True, stop=True
+                )
 
         def codes_and_scales(name, width):
             codes = codes_pool.tile([P, width], U32, name=name + "_codes", align_bytes=64)
@@ -333,7 +342,11 @@ def tile_transposedattentiontransformer_pa_kernel(tc, h, w_qk, w_q_norm, w_k_nor
             if n == -MATMUL_AHEAD:
                 broadcast_gains()
             tiles = tiles_of_step[n]
+            if n == FIRST_STEP:
+                keep_clock(BANK, times=5)
             in_psum = [transpose_row_tile(key) for key in tiles]
+            if n < -MATMUL_AHEAD - 1:
+                keep_clock(320, times=len(tiles))
             newly_copied = []
             squares_left = n + 1 < N_BANKS
 

@@ -83,6 +83,8 @@ def tile_transposedattentiontransformer_pa_kernel(tc, h, w_qk, w_q_norm, w_k_nor
         row_tiles = [key for n in sorted(tiles_of_step) for key in tiles_of_step[n]]
         assert len(row_tiles) == ROW_TILES
 
+        zeros = const.tile([P, BANK], BF16)
+        nc.vector.memset(zeros[:], 0.0)
         rows_sb = {}
         gain_rows = const.tile([P, 2 * D], BF16)
         nc.vector.memset(gain_rows[:], 0.0)
@@ -108,8 +110,6 @@ def tile_transposedattentiontransformer_pa_kernel(tc, h, w_qk, w_q_norm, w_k_nor
         nc.scalar.activation(out=warm[:], in_=eps[:], func=ACT.Abs_reciprocal_sqrt)
         ones = const.tile([P, P], BF16)
         nc.vector.memset(ones[:], 1.0)
-        zeros = const.tile([P, BANK], BF16)
-        nc.vector.memset(zeros[:], 0.0)
         gains = const.tile([P, 2 * D], F32)
 
         def broadcast_gains():
@@ -121,7 +121,7 @@ def tile_transposedattentiontransformer_pa_kernel(tc, h, w_qk, w_q_norm, w_k_nor
             unread = psum.tile([P, BANK], F32, tag="bank")
             for i in range(times):
                 nc.tensor.matmul(
-                    out=unread[:, 0:columns], lhsT=ones[:], rhs=zeros[:, 0:columns], start=True, stop=True
+                    out=unread[:, 0:columns], lhsT=zeros[:, 0:P], rhs=zeros[:, 0:columns], start=True, stop=True
                 )
 
         def codes_and_scales(name, width):
@@ -343,10 +343,10 @@ def tile_transposedattentiontransformer_pa_kernel(tc, h, w_qk, w_q_norm, w_k_nor
                 broadcast_gains()
             tiles = tiles_of_step[n]
             if n == FIRST_STEP:
-                keep_clock(BANK, times=5)
+                keep_clock(BANK, times=6)
             in_psum = [transpose_row_tile(key) for key in tiles]
             if n < -MATMUL_AHEAD - 1:
-                keep_clock(320, times=len(tiles))
+                keep_clock(384, times=len(tiles))
             newly_copied = []
             squares_left = n + 1 < N_BANKS
 

@@ -41,7 +41,7 @@ SINGLE_TILES = TOKEN_TILES + 2
 PAIRS_FIRST_STEP = FIRST_STEP + SINGLE_TILES
 PAIRS_LAST_STEP = HALF_TILES - MATMUL_AHEAD - 2
 LATE_FIRST_STEP = PAIRS_LAST_STEP + 1
-GPSIMD_CHANNELS = 92
+GPSIMD_CHANNELS = 96
 ROW_TILES_DONE = 2 * HALF_TILES
 
 FLOPS = 2 * BATCH * TOKENS * CHANNELS * 2 * HEADS * D + 2 * BATCH * HEADS * D * D * TOKENS

@@ -79,7 +79,7 @@ def tile_transposedattentiontransformer_pa_kernel(tc, h, w_qk, w_q_norm, w_k_nor
                 step = min(PAIRS_FIRST_STEP + 2 * ((t - SINGLE_TILES) // 2), PAIRS_LAST_STEP)
             tiles_of_step[step].append(key)
         for i in range(HALF_TILES):
-            tiles_of_step[LATE_FIRST_STEP + 8 * i // 5].append(w_tile(2 * HALF_TILES + i))
+            tiles_of_step[LATE_FIRST_STEP + i // 2 * 3 + i % 2].append(w_tile(2 * HALF_TILES + i))
         row_tiles = [key for n in sorted(tiles_of_step) for key in tiles_of_step[n]]
         assert len(row_tiles) == ROW_TILES
 
@@ -346,7 +346,7 @@ def tile_transposedattentiontransformer_pa_kernel(tc, h, w_qk, w_q_norm, w_k_nor
                 keep_clock(BANK, times=6)
             in_psum = [transpose_row_tile(key) for key in tiles]
             if n < -MATMUL_AHEAD - 1:
-                keep_clock(384, times=len(tiles))
+                keep_clock(352, times=len(tiles))
             newly_copied = []
             squares_left = n + 1 < N_BANKS
 
@@ -357,19 +357,21 @@ def tile_transposedattentiontransformer_pa_kernel(tc, h, w_qk, w_q_norm, w_k_nor
                 deferred = None
             if is_bank(n):
                 normalise(n)
+            if is_bank(n - QUANTISE_LAG):
+                quantise(n - QUANTISE_LAG)
             for key, grouped in copied:
                 quantise_row_tile(key, grouped)
-            vector_helps = not squares_left or (n % 3 != 0 if n < ROW_TILES_DONE else n % 3 == 0)
+            m = n - SCORES_LAG - 1
+            scores_finished = is_bank_of_k(m) and banks[m][3] == last_head
+            if scores_finished:
+                softmax_max(*banks[m][:2])
+            vector_helps = not squares_left or n < ROW_TILES_DONE or n % 3 == 0
             if is_bank(n - 1) and vector_helps:
                 regroup(n - 1, nc.vector.tensor_copy, GPSIMD_CHANNELS, D)
             for i, (key, bank) in enumerate(zip(tiles, in_psum)):
                 if on_vector(n, i):
                     newly_copied.append((key, copy_row_tile(bank, nc.vector.tensor_copy)))
-            if is_bank(n - QUANTISE_LAG):
-                quantise(n - QUANTISE_LAG)
-            m = n - SCORES_LAG - 1
-            if is_bank_of_k(m) and banks[m][3] == last_head:
-                softmax_max(*banks[m][:2])
+            if scores_finished:
                 softmax_negate(*banks[m][:2])
 
             if is_bank(n + MATMUL_AHEAD):

from contextlib import ExitStack

import concourse.mybir as mybir
from concourse.masks import make_identity

F32 = mybir.dt.float32
BF16 = mybir.dt.bfloat16
U32 = mybir.dt.uint32
U8 = mybir.dt.uint8
FP8X4 = mybir.dt.float8_e4m3fn_x4
ACT = mybir.ActivationFunctionType
ALU = mybir.AluOpType
AXIS = mybir.AxisListType

P = 128
PACK = 4
BATCH = 2
TOKENS = 512
CHANNELS = 1024
PASSES = CHANNELS // (P * PACK)
HEADS = 8
D = 128
EPS = 1e-5
SOFTMAX_SCALE = D**-0.5

BANK = 512
TOKEN_TILES = TOKENS // P
WORDS = CHANNELS // 2
HEADS_PER_BANK = BANK // D
HALVES = HEADS // HEADS_PER_BANK

N_BANKS = 2 * HEADS * BATCH
ROW_TILES = (BATCH * TOKENS + 2 * HEADS * D) // P
HALF_TILES = 2 * HEADS_PER_BANK

MATMUL_AHEAD = 2
QUANTISE_LAG = 2
SCORES_LAG = QUANTISE_LAG + 2
FIRST_STEP = -9
SINGLE_TILES = TOKEN_TILES + 2
PAIRS_FIRST_STEP = FIRST_STEP + SINGLE_TILES
PAIRS_LAST_STEP = HALF_TILES - MATMUL_AHEAD - 2
LATE_FIRST_STEP = PAIRS_LAST_STEP + 1
GPSIMD_CHANNELS = 96
ROW_TILES_DONE = 2 * HALF_TILES

FLOPS = 2 * BATCH * TOKENS * CHANNELS * 2 * HEADS * D + 2 * BATCH * HEADS * D * D * TOKENS


def tile_transposedattentiontransformer_pa_kernel(tc, h, w_qk, w_q_norm, w_k_norm, out):
    nc = tc.nc
    with ExitStack() as ctx:
        const = ctx.enter_context(tc.tile_pool(name="const", bufs=1))
        rows_pool = ctx.enter_context(tc.tile_pool(name="rows", bufs=1))
        codes_pool = ctx.enter_context(tc.tile_pool(name="codes", bufs=1))
        work = ctx.enter_context(tc.tile_pool(name="work", bufs=8))
        psum = ctx.enter_context(tc.psum_pool(name="psum", bufs=8))
        ctx.enter_context(tc.manual_schedule())

        banks = []
        for half in range(HALVES):
            for b in range(BATCH):
                for is_k in range(2):
                    for head in range(HEADS_PER_BANK):
                        banks.append((b, half, is_k, head))
        assert len(banks) == N_BANKS

        def w_tile(n):
            half, is_k, head = banks[n][1:]
            return ("w", is_k, half * HEADS_PER_BANK + head)

        tiles_of_step = {n: [] for n in range(FIRST_STEP, N_BANKS)}
        early_tiles = [w_tile(0)] + [("h", 0, j) for j in range(TOKEN_TILES)]
        early_tiles += [w_tile(n) for n in range(1, HALF_TILES)] + [("h", 1, j) for j in range(TOKEN_TILES)]
        for t, key in enumerate(early_tiles):
            if t < SINGLE_TILES:
                step = FIRST_STEP + t
            else:
                step = min(PAIRS_FIRST_STEP + 2 * ((t - SINGLE_TILES) // 2), PAIRS_LAST_STEP)
            tiles_of_step[step].append(key)
        for i in range(HALF_TILES):
            tiles_of_step[LATE_FIRST_STEP + i // 2 * 3 + i % 2].append(w_tile(2 * HALF_TILES + i))
        row_tiles = [key for n in sorted(tiles_of_step) for key in tiles_of_step[n]]
        assert len(row_tiles) == ROW_TILES

        zeros = const.tile([P, BANK], BF16)
        nc.vector.memset(zeros[:], 0.0)
        rows_sb = {}
        gain_rows = const.tile([P, 2 * D], BF16)
        nc.vector.memset(gain_rows[:], 0.0)
        for t, key in enumerate(row_tiles):
            kind, group, i = key
            rows = rows_pool.tile([P, CHANNELS], BF16, name="rows%d" % t)
            if kind == "w":
                first = (group * HEADS + i) * D
                source = w_qk[first : first + P, :]
            else:
                source = h[group].rearrange("(p j) c -> j p c", j=TOKEN_TILES)[i]
            nc.sync.dma_start(out=rows[:], in_=source)
            rows_sb[key] = rows
            if key == ("h", 0, TOKEN_TILES - 1):
                nc.sync.dma_start(out=gain_rows[0:1, 0:D], in_=w_q_norm.rearrange("(o d) -> o d", o=1))
                nc.sync.dma_start(out=gain_rows[0:1, D : 2 * D], in_=w_k_norm.rearrange("(o d) -> o d", o=1))

        identity = const.tile([P, P], F32)
        make_identity(nc, identity[:])
        eps = const.tile([P, 1], F32)
        nc.vector.memset(eps[:], EPS)
        warm = const.tile([P, 1], F32)
        nc.scalar.activation(out=warm[:], in_=eps[:], func=ACT.Abs_reciprocal_sqrt)
        ones = const.tile([P, P], BF16)
        nc.vector.memset(ones[:], 1.0)
        gains = const.tile([P, 2 * D], F32)

        def broadcast_gains():
            gain_ps = psum.tile([P, BANK], F32, tag="bank")
            nc.tensor.matmul(out=gain_ps[:, 0 : 2 * D], lhsT=ones[:], rhs=gain_rows[:], start=True, stop=True)
            nc.vector.tensor_copy(out=gains[:], in_=gain_ps[:, 0 : 2 * D])

        def keep_clock(columns, times=1):
            unread = psum.tile([P, BANK], F32, tag="bank")
            for i in range(times):
                nc.tensor.matmul(
                    out=unread[:, 0:columns], lhsT=zeros[:, 0:P], rhs=zeros[:, 0:columns], start=True, stop=True
                )

        def codes_and_scales(name, width):
            codes = codes_pool.tile([P, width], U32, name=name + "_codes", align_bytes=64)
            scales = codes_pool.tile([P, width], U8, name=name + "_scales", align_bytes=64)
            return codes, scales

        rows_mx = {key: codes_and_scales("rows%d" % t, PASSES * P) for t, key in enumerate(row_tiles)}
        qk_mx = [codes_and_scales("qk%d" % n, D) for n in range(N_BANKS)]

        def transpose_row_tile(key):
            words = rows_sb[key][:].bitcast(F32)
            bank = psum.tile([P, BANK], F32, tag="bank")
            for block in range(WORDS // P):
                cols = slice(block * P, (block + 1) * P)
                nc.tensor.transpose(bank[:, cols], words[:, cols], identity[:])
            return bank

        def copy_row_tile(bank, copy):
            grouped = work.tile([P, PASSES * P * PACK], BF16, name="grouped", align_bytes=64)
            copy(
                out=grouped[:].bitcast(F32).rearrange("p (g r u) -> p g r u", g=PASSES, u=2),
                in_=bank[:].rearrange("p (g u r) -> p g r u", g=PASSES, u=2),
            )
            return grouped

        def quantise_row_tile(key, grouped):
            codes, scales = rows_mx[key]
            nc.vector.quantize_mx(out=codes[:].bitcast(FP8X4), scales=scales[:], in_=grouped[:])

        raw_banks = {}
        sum_sq_tiles = {}
        inv_rms_tiles = {}
        normed = {}
        regrouped = {}

        def first_matmul(n, tokens=range(TOKEN_TILES)):
            b = banks[n][0]
            w_codes, w_scales = rows_mx[w_tile(n)]
            if n not in raw_banks:
                raw_banks[n] = psum.tile([P, BANK], F32, name="raw", tag="bank")
            for j in tokens:
                h_codes, h_scales = rows_mx[("h", b, j)]
                for g in range(PASSES):
                    cols = slice(g * P, (g + 1) * P)
                    nc.tensor.matmul_mx(
                        out=raw_banks[n][:, j * D : (j + 1) * D],
                        lhsT=h_codes[:, cols].bitcast(FP8X4),
                        lhsT_scale=h_scales[:, cols],
                        rhs=w_codes[:, cols].bitcast(FP8X4),
                        rhs_scale=w_scales[:, cols],
                        start=(g == 0),
                        stop=(g == PASSES - 1),
                    )

        def sum_squares(n, tokens=range(TOKEN_TILES)):
            if n not in sum_sq_tiles:
                sum_sq_tiles[n] = work.tile([P, TOKEN_TILES], F32, name="sum_sq")
            for j in tokens:
                squares = work.tile([P, D], BF16, name="squares")
                nc.scalar.activation(
                    out=squares[:],
                    in_=raw_banks[n][:, j * D : (j + 1) * D],
                    func=ACT.Square,
                    accum_out=sum_sq_tiles[n][:, j : j + 1],
                )

        def inverse_rms(n):
            inv_rms_tiles[n] = work.tile([P, TOKEN_TILES], F32, name="inv_rms")
            nc.scalar.activation(
                out=inv_rms_tiles[n][:],
                in_=sum_sq_tiles[n][:],
                func=ACT.Abs_reciprocal_sqrt,
                scale=1.0 / D,
                bias=eps[:, 0:1],
            )

        def normalise(n):
            is_k = banks[n][2]
            normed[n] = work.tile([P, BANK], BF16, name="normed")
            for j in range(TOKEN_TILES):
                nc.vector.scalar_tensor_tensor(
                    out=normed[n][:, j * D : (j + 1) * D],
                    in0=raw_banks[n][:, j * D : (j + 1) * D],
                    scalar=inv_rms_tiles[n][:, j : j + 1],
                    in1=gains[:, is_k * D : (is_k + 1) * D],
                    op0=ALU.mult,
                    op1=ALU.mult,
                )
            regrouped[n] = work.tile([P, D * PACK], BF16, name="regrouped", align_bytes=64)

        def gpsimd_copy(out, in_):
            nc.gpsimd.tensor_scalar(out=out, in0=in_, scalar1=1.0, scalar2=0.0, op0=ALU.mult, op1=ALU.add)

        def regroup(n, copy, first, last):
            chans = slice(first, last)
            copy(
                out=regrouped[n][:, first * PACK : last * PACK].rearrange("p (c i j) -> p c j i", i=4, j=TOKEN_TILES),
                in_=normed[n][:].rearrange("p (j c) -> p j c", j=TOKEN_TILES)[:, :, chans].rearrange(
                    "p j (c i) -> p c j i", i=4
                ),
            )

        def quantise(n):
            codes, scales = qk_mx[n]
            nc.vector.quantize_mx(out=codes[:].bitcast(FP8X4), scales=scales[:], in_=regrouped[n][:])

        scores = {}
        head_scores = {}
        row_max = {}
        neg_max = {}

        def second_matmul(n):
            b, half, is_k, head = banks[n]
            q_codes, q_scales = qk_mx[banks.index((b, half, 0, head))]
            k_codes, k_scales = qk_mx[n]
            apart = n >= N_BANKS - HEADS_PER_BANK
            if head == 0 or apart:
                bank_of_scores = psum.tile([P, BANK], F32, name="scores", tag="bank")
            if head == 0:
                scores[(b, half)] = bank_of_scores
            first = 0 if apart else head * D
            head_scores[(b, half, head)] = (bank_of_scores if apart else scores[(b, half)])[:, first : first + D]
            nc.tensor.matmul_mx(
                out=head_scores[(b, half, head)],
                lhsT=q_codes[:].bitcast(FP8X4),
                lhsT_scale=q_scales[:],
                rhs=k_codes[:].bitcast(FP8X4),
                rhs_scale=k_scales[:],
                start=True,
                stop=True,
            )

        def softmax_max(b, half, heads=slice(0, HEADS_PER_BANK)):
            count = heads.stop - heads.start
            if (b, half) not in row_max:
                row_max[(b, half)] = work.tile([P, HEADS_PER_BANK], F32, name="row_max")
                neg_max[(b, half)] = work.tile([P, HEADS_PER_BANK], F32, name="neg_max")
            nc.vector.reduce_max(
                out=row_max[(b, half)][:, heads],
                in_=scores[(b, half)][:, heads.start * D : heads.stop * D].rearrange("p (g e) -> p g e", g=count),
                axis=AXIS.X,
            )

        def softmax_negate(b, half, heads=slice(0, HEADS_PER_BANK)):
            nc.vector.tensor_scalar_mul(out=neg_max[(b, half)][:, heads], in0=row_max[(b, half)][:, heads], scalar1=-SOFTMAX_SCALE)

        def softmax_shift(b, half, head):
            if (b, half) not in neg_max:
                neg_max[(b, half)] = work.tile([P, HEADS_PER_BANK], F32, name="neg_max")
            junk = work.tile([P, D], F32, name="junk")
            nc.vector.tensor_scalar(
                out=junk[:],
                in0=head_scores[(b, half, head)],
                scalar1=-SOFTMAX_SCALE,
                scalar2=None,
                op0=ALU.mult,
                op1=ALU.min,
                accum_out=neg_max[(b, half)][:, head : head + 1],
            )

        weights = {}
        sums = {}
        inv_sums = {}

        def softmax_exp(b, half, heads=slice(0, HEADS_PER_BANK)):
            key = (b, half)
            if key not in weights:
                weights[key] = work.tile([P, BANK], F32, name="weights")
                sums[key] = work.tile([P, HEADS_PER_BANK], F32, name="sums")
                inv_sums[key] = work.tile([P, HEADS_PER_BANK], F32, name="inv_sums")
            for head in range(heads.start, heads.stop):
                cols = slice(head * D, (head + 1) * D)
                nc.scalar.activation(
                    out=weights[key][:, cols],
                    in_=head_scores[(b, half, head)],
                    func=ACT.Exp,
                    scale=SOFTMAX_SCALE,
                    bias=neg_max[key][:, head : head + 1],
                    accum_out=sums[key][:, head : head + 1],
                )

        def softmax_recip(b, half, heads=slice(0, HEADS_PER_BANK)):
            key = (b, half)
            nc.vector.reciprocal(out=inv_sums[key][:, heads], in_=sums[key][:, heads])

        def softmax_mul(b, half, heads=slice(0, HEADS_PER_BANK)):
            key = (b, half)
            for head in range(heads.start, heads.stop):
                cols = slice(head * D, (head + 1) * D)
                nc.vector.tensor_scalar_mul(
                    out=weights[key][:, cols], in0=weights[key][:, cols], scalar1=inv_sums[key][:, head : head + 1]
                )
            first = half * HEADS_PER_BANK
            nc.sync.dma_start(
                out=out[b, first + heads.start : first + heads.stop].rearrange("g d e -> d g e"),
                in_=weights[key][:, heads.start * D : heads.stop * D].rearrange("p (g e) -> p g e", g=heads.stop - heads.start),
            )

        def is_bank(n):
            return 0 <= n < N_BANKS

        def is_bank_of_k(n):
            return is_bank(n) and banks[n][2] == 1

        last_banks = range(N_BANKS - HEADS_PER_BANK, N_BANKS)
        scores_done = [banks[n][:2] for n in range(N_BANKS) if is_bank_of_k(n) and banks[n][3] == HEADS_PER_BANK - 1]
        early_scores, last_scores = scores_done[:-1], scores_done[-1]
        last_head = HEADS_PER_BANK - 1
        exps = list(early_scores)

        deferred = None
        def on_vector(n, i):
            return i == 1 and n < PAIRS_LAST_STEP

        copied = []
        for n in range(FIRST_STEP, N_BANKS):
            if n == -MATMUL_AHEAD:
                broadcast_gains()
            tiles = tiles_of_step[n]
            if n == FIRST_STEP:
                keep_clock(BANK, times=6)
            in_psum = [transpose_row_tile(key) for key in tiles]
            if n < -MATMUL_AHEAD - 1:
                keep_clock(352, times=len(tiles))
            newly_copied = []
            squares_left = n + 1 < N_BANKS

            if is_bank(n + 1):
                sum_squares(n + 1, [0])
            if deferred is not None:
                inverse_rms(deferred)
                deferred = None
            if is_bank(n):
                normalise(n)
            if is_bank(n - QUANTISE_LAG):
                quantise(n - QUANTISE_LAG)
            for key, grouped in copied:
                quantise_row_tile(key, grouped)
            m = n - SCORES_LAG - 1
            scores_finished = is_bank_of_k(m) and banks[m][3] == last_head
            if scores_finished:
                softmax_max(*banks[m][:2])
            vector_helps = not squares_left or n < ROW_TILES_DONE or n % 3 == 0
            if is_bank(n - 1) and vector_helps:
                regroup(n - 1, nc.vector.tensor_copy, GPSIMD_CHANNELS, D)
            for i, (key, bank) in enumerate(zip(tiles, in_psum)):
                if on_vector(n, i):
                    newly_copied.append((key, copy_row_tile(bank, nc.vector.tensor_copy)))
            if scores_finished:
                softmax_negate(*banks[m][:2])

            if is_bank(n + MATMUL_AHEAD):
                first_matmul(n + MATMUL_AHEAD)
            if is_bank_of_k(n - SCORES_LAG):
                second_matmul(n - SCORES_LAG)

            if is_bank(n + 1):
                sum_squares(n + 1, [1, 2, 3])
            for i, (key, bank) in enumerate(zip(tiles, in_psum)):
                if on_vector(n, i):
                    continue
                newly_copied.append((key, copy_row_tile(bank, nc.scalar.copy)))
            if is_bank(n - 1) and not vector_helps:
                regroup(n - 1, nc.scalar.copy, GPSIMD_CHANNELS, D)
            if is_bank(n + 1):
                if tiles or n + 2 >= N_BANKS:
                    inverse_rms(n + 1)
                else:
                    deferred = n + 1
            elif n >= N_BANKS - 1 and exps:
                softmax_exp(*exps.pop(0))

            if is_bank(n - 1):
                regroup(n - 1, gpsimd_copy, 0, GPSIMD_CHANNELS)

            copied = newly_copied

        most = slice(0, last_head)
        one = slice(last_head, HEADS_PER_BANK)
        n = N_BANKS - 1
        d0, d1, d2 = early_scores
        for key in exps:
            softmax_exp(*key)
        second_matmul(n - 3)
        second_matmul(n - 2)
        regroup(n, nc.vector.tensor_copy, 0, D)
        quantise(n - 1)
        second_matmul(n - 1)
        quantise(n)
        second_matmul(n)
        softmax_recip(*d0)
        softmax_shift(*last_scores, 0)
        softmax_mul(*d0)
        softmax_shift(*last_scores, 1)
        softmax_recip(*d1)
        softmax_shift(*last_scores, 2)
        softmax_exp(*last_scores, heads=most)
        softmax_mul(*d1)
        softmax_shift(*last_scores, 3)
        softmax_exp(*last_scores, heads=one)
        softmax_recip(*d2)
        softmax_mul(*d2)
        softmax_recip(*last_scores, heads=most)
        softmax_mul(*last_scores, heads=most)
        softmax_recip(*last_scores, heads=one)
        softmax_mul(*last_scores, heads=one)
